import numpy as np
import ml_dtypes


def mxq(x, axis, fmt="e4m3"):
    dtype, down = {"e4m3": (ml_dtypes.float8_e4m3fn, 7), "e5m2": (ml_dtypes.float8_e5m2, 14)}[fmt]
    v = np.moveaxis(np.asarray(x, np.float32).astype(ml_dtypes.bfloat16).astype(np.float64), axis, -1)
    blocks = v.reshape(v.shape[:-1] + (-1, 32))
    amax = np.abs(blocks).max(-1, keepdims=True)
    byte = np.maximum(np.where(amax > 0, np.frexp(amax)[1] - 1 + 127, 0) - down, 1)
    scale = np.exp2(byte - 127.0)
    codes = (blocks / scale).astype(np.float32).astype(dtype).astype(np.float64)
    return np.moveaxis((codes * scale).reshape(v.shape), -1, axis)


WIDE = False


def mx_kscale(k):
    if not WIDE:
        return np.ones(k)
    levels = np.array([10, -10, 5, -5, 0])
    a = np.random.permutation(np.resize(levels, k // 512 * 4)).reshape(k // 512, 4)
    idx = np.arange(k)
    return np.exp2(a[idx // 512, idx % 128 // 32])


BF16 = ml_dtypes.bfloat16


def bf(x):
    return np.asarray(x, np.float32).astype(BF16)


def f64(x):
    return np.asarray(x).astype(np.float64)


B, S, D, A, H = 4, 1024, 512, 512, 4
HD = A // H


def setup_inputs():
    s = mx_kscale(D)
    return {"q_rot": bf(np.random.standard_normal((B, S, A)) * 1.5 / np.sqrt(HD)),
            "k_rot": bf(np.random.standard_normal((B, S, A)) * 0.5),
            "hidden_states": bf(np.random.standard_normal((B, S, D)) * s),
            "Wv": bf(np.random.standard_normal((A, D)) * 0.5 / np.sqrt(D) / s),
            "bv": bf(np.random.standard_normal(A) * 2.0 * H / S)}


def reference(q_rot, k_rot, hidden_states, Wv, bv):
    v = (mxq(f64(hidden_states), 2, "e4m3") @ mxq(f64(Wv), 1, "e4m3").T) + f64(bv)
    qh = f64(q_rot).reshape(B, S, H, HD).transpose(0, 2, 1, 3)
    kh = f64(k_rot).reshape(B, S, H, HD).transpose(0, 2, 1, 3)
    vh = v.reshape(B, S, H, HD).transpose(0, 2, 1, 3)
    scores = qh @ kh.transpose(0, 1, 3, 2)
    e = np.exp(scores - scores.max(1, keepdims=True))
    probs = e / e.sum(1, keepdims=True)
    ctx = mxq(probs, 3, "e4m3") @ mxq(vh, 2, "e4m3")
    return ctx.reshape(B, S, A)

@@ -1,0 +1,299 @@
+from contextlib import ExitStack
+
+import concourse.mybir as mybir
+from concourse.masks import make_identity
+
+B, S, D, A, H = 4, 1024, 512, 512, 4
+HD = A // H
+FLOPS = 2 * B * S * D * A + 2 * 2 * B * H * S * S * HD
+
+F32 = mybir.dt.float32
+BF16 = mybir.dt.bfloat16
+U32 = mybir.dt.uint32
+U8 = mybir.dt.uint8
+FP8X4 = mybir.dt.float8_e4m3fn_x4
+ACT = mybir.ActivationFunctionType
+ALU = mybir.AluOpType
+
+P = 128
+PACK = 4
+K_PASS = P * PACK
+G = S // K_PASS
+TILES = G * PACK
+UNIT = P * PACK
+UNITS_PER_BATCH = TILES * G
+GROUP = 4
+LAG = 7
+ODD_FIRST = (1, 3, 0, 2)
+
+
+def tile_sparseattention_pb_t_kernel(tc, q_rot, k_rot, hidden_states, Wv, bv, out):
+    nc = tc.nc
+    units = [(b, gi, ti, g) for b in range(B) for gi in range(G) for ti in range(PACK) for g in range(G)]
+    n_units = len(units)
+
+    with ExitStack() as stack:
+        const = stack.enter_context(tc.tile_pool(name="const", bufs=1))
+        raw_pool = stack.enter_context(tc.tile_pool(name="raw", bufs=G))
+        prep = stack.enter_context(tc.tile_pool(name="prep", bufs=1))
+        per_batch = stack.enter_context(tc.tile_pool(name="per_batch", bufs=2))
+        soft = stack.enter_context(tc.tile_pool(name="soft", bufs=2))
+        exp_pool = stack.enter_context(tc.tile_pool(name="exp", bufs=LAG + 1))
+        sum_pool = stack.enter_context(tc.tile_pool(name="sum", bufs=3))
+        code_pool = stack.enter_context(tc.tile_pool(name="codes", bufs=4))
+        out_pool = stack.enter_context(tc.tile_pool(name="out", bufs=2))
+        score_ps = stack.enter_context(tc.psum_pool(name="score_ps", bufs=5))
+        ctx_ps_pool = stack.enter_context(tc.psum_pool(name="ctx_ps", bufs=1))
+        prep_ps = stack.enter_context(tc.psum_pool(name="prep_ps", bufs=2))
+        stack.enter_context(tc.manual_schedule())
+
+        ident_bf = const.tile([P, P], BF16)
+        make_identity(nc, ident_bf[:])
+        ident_f32 = const.tile([P, P], F32)
+        make_identity(nc, ident_f32[:])
+        bias_rows = const.tile([P, A], BF16)
+        wv_codes = const.tile([P, A], U32, align_bytes=64)
+        wv_scales = const.tile([P, A], U8, align_bytes=64)
+
+        raws = {}
+        turned_qk = {}
+        hs_mx = {}
+        grouped_hs = {}
+        v_banks = {}
+        grouped_v = {}
+        v_mx = {}
+        banks = {}
+        odd_copies = {}
+        exps = {}
+        sums = {}
+        probs_bf = {}
+        probs_mx = {}
+        staged = {}
+
+        def load_batch(b):
+            for g in range(G):
+                for name, x in (("k", k_rot), ("q", q_rot), ("h", hidden_states)):
+                    raw = raw_pool.tile([P, PACK, D], BF16, tag="raw_" + name, name="raw_" + name)
+                    nc.sync.dma_start(out=raw[:], in_=x[b].rearrange("(g p t) c -> g p t c", g=G, p=P)[g])
+                    raws[(name, b, g)] = raw
+
+        def turn_words(raw, grouped, pair):
+            words = raw[:].bitcast(F32)
+            turned = prep_ps.tile([P, 2, 2, P], F32, tag="prep")
+            for n in range(2):
+                for u in range(2):
+                    nc.tensor.transpose(turned[:, n, u, :], words[:, 2 * pair + n, u * P : (u + 1) * P], ident_f32[:])
+            nc.scalar.copy(
+                out=grouped[:].bitcast(F32)[:, 2 * pair : 2 * pair + 2, :, :],
+                in_=turned[:].rearrange("p n u r -> p n r u"),
+            )
+
+        def turn_heads(b, tile_index):
+            g, t = divmod(tile_index, PACK)
+            if tile_index == 0:
+                qk = per_batch.tile([P, G, PACK, 2, H, P], BF16, tag="turned_qk")
+                turned_qk[b] = qk
+            turned = prep_ps.tile([P, 2, H, P], BF16, tag="prep")
+            for which, name in enumerate(("q", "k")):
+                for h in range(H):
+                    nc.tensor.transpose(turned[:, which, h, :], raws[(name, b, g)][:, t, h * HD : (h + 1) * HD], ident_bf[:])
+            nc.scalar.copy(out=turned_qk[b][:, g, t, :, :, :], in_=turned[:])
+
+        def quantise_grouped(grouped, codes, scales):
+            nc.vector.quantize_mx(
+                out=codes.bitcast(FP8X4), scales=scales, in_=grouped[:].rearrange("p n r t -> p (n r t)")
+            )
+
+        def project_v(b, g, h):
+            codes, scales = hs_mx[b]
+            bank = prep_ps.tile([P, PACK, HD], F32, tag="prep")
+            for t in range(PACK):
+                nc.tensor.matmul_mx(
+                    out=bank[:, t, :],
+                    lhsT=codes[:, g, t * P : (t + 1) * P].bitcast(FP8X4),
+                    lhsT_scale=scales[:, g, t * P : (t + 1) * P],
+                    rhs=wv_codes[:, h * HD : (h + 1) * HD].bitcast(FP8X4),
+                    rhs_scale=wv_scales[:, h * HD : (h + 1) * HD],
+                    start=True,
+                    stop=True,
+                )
+            v_banks[(b, g, h)] = bank
+
+        def prepare_early(b, step):
+            if step < TILES:
+                turn_heads(b, step)
+            if step < 2 * G:
+                g, pair = divmod(step, 2)
+                if pair == 0:
+                    grouped = prep.tile([P, PACK, P, PACK], BF16, tag="grouped", align_bytes=64)
+                    grouped_hs[(b, g)] = grouped
+                turn_words(raws[("h", b, g)], grouped_hs[(b, g)], pair)
+            if step >= TILES:
+                g, h = divmod(step - TILES, H)
+                project_v(b, g, h)
+
+        def prepare_late(b, step):
+            if step < 2 * G and step % 2 == 1:
+                g = step // 2
+                if g == 0:
+                    hs_codes = prep.tile([P, G, K_PASS], U32, align_bytes=64)
+                    hs_scales = prep.tile([P, G, K_PASS], U8, align_bytes=64)
+                    hs_mx[b] = (hs_codes, hs_scales)
+                quantise_grouped(grouped_hs[(b, g)], hs_mx[b][0][:, g, :], hs_mx[b][1][:, g, :])
+            if step >= TILES:
+                g, h = divmod(step - TILES, H)
+                if h == 0:
+                    grouped = prep.tile([P, H, HD, PACK], BF16, tag="grouped_v", align_bytes=64)
+                    grouped_v[(b, g)] = grouped
+                nc.vector.tensor_tensor(
+                    out=grouped_v[(b, g)][:, h, :, :],
+                    in0=v_banks[(b, g, h)][:].rearrange("p t a -> p a t"),
+                    in1=bias_rows[:, h * HD : (h + 1) * HD].unsqueeze(2).to_broadcast([P, HD, PACK]),
+                    op=ALU.add,
+                )
+                if h == H - 1:
+                    if g == 0:
+                        v_codes = per_batch.tile([P, G, A], U32, align_bytes=64)
+                        v_scales = per_batch.tile([P, G, A], U8, align_bytes=64)
+                        v_mx[b] = (v_codes, v_scales)
+                    quantise_grouped(grouped_v[(b, g)], v_mx[b][0][:, g, :], v_mx[b][1][:, g, :])
+
+        def scores(k):
+            b, gi, ti, g = units[k]
+            qk = turned_qk[b]
+            banks[k] = {}
+            for h in ODD_FIRST:
+                bank = score_ps.tile([P, P, PACK], F32, tag="scores")
+                for t in range(PACK):
+                    nc.tensor.matmul(
+                        out=bank[:, :, t], lhsT=qk[:, g, t, 1, h, :], rhs=qk[:, gi, ti, 0, h, :], start=True, stop=True
+                    )
+                banks[k][h] = bank[:].rearrange("p i t -> p (i t)")
+
+        def copy_odd_heads(k):
+            odd = soft.tile([P, 2, UNIT], BF16, tag="odd")
+            for n in range(2):
+                nc.scalar.copy(out=odd[:, n, :], in_=banks[k][2 * n + 1])
+            odd_copies[k] = odd
+
+        def subtract_top(k):
+            pair_top = soft.tile([P, 2, UNIT], BF16, tag="pair_top")
+            for n in range(2):
+                nc.vector.tensor_tensor(out=pair_top[:, n, :], in0=banks[k][2 * n], in1=odd_copies[k][:, n, :], op=ALU.max)
+            top = soft.tile([P, UNIT], BF16, tag="top")
+            nc.vector.tensor_tensor(out=top[:], in0=pair_top[:, 0, :], in1=pair_top[:, 1, :], op=ALU.max)
+            shifted = exp_pool.tile([P, H, UNIT], F32, tag="exps")
+            for h in ODD_FIRST:
+                nc.vector.tensor_tensor(out=shifted[:, h, :], in0=banks[k][h], in1=top[:], op=ALU.subtract)
+            exps[k] = shifted
+
+        def exponentials(k):
+            flat = exps[k][:].rearrange("p h x -> p (h x)")
+            nc.scalar.activation(out=flat, in_=flat, func=ACT.Exp)
+
+        def sum_heads(k):
+            group, member = divmod(k, GROUP)
+            if member == 0:
+                total = sum_pool.tile([P, GROUP, UNIT], F32, tag="sums")
+                sums[group] = total
+            half = soft.tile([P, 2, UNIT], F32, tag="half")
+            nc.gpsimd.tensor_tensor(out=half[:], in0=exps[k][:, 0:2, :], in1=exps[k][:, 2:4, :], op=ALU.add)
+            nc.gpsimd.tensor_tensor(out=sums[group][:, member, :], in0=half[:, 0, :], in1=half[:, 1, :], op=ALU.add)
+
+        def log_of_sums(group):
+            flat = sums[group][:].rearrange("p m x -> p (m x)")
+            nc.scalar.activation(out=flat, in_=flat, func=ACT.Ln)
+
+        def reciprocal_of_sums(group):
+            flat = sums[group][:].rearrange("p m x -> p (m x)")
+            nc.scalar.activation(out=flat, in_=flat, func=ACT.Exp, scale=-1.0)
+
+        def normalise(k):
+            group, member = divmod(k, GROUP)
+            probs = soft.tile([P, H, UNIT], BF16, tag="probs", align_bytes=64)
+            nc.vector.tensor_tensor(
+                out=probs[:],
+                in0=exps[k][:],
+                in1=sums[group][:, member, :].unsqueeze(1).to_broadcast([P, H, UNIT]),
+                op=ALU.mult,
+            )
+            probs_bf[k] = probs
+
+        def quantise_probs(k):
+            codes = code_pool.tile([P, H * P], U32, tag="probs_codes", align_bytes=64)
+            scales = code_pool.tile([P, H * P], U8, tag="probs_scales", align_bytes=64)
+            nc.vector.quantize_mx(
+                out=codes[:].bitcast(FP8X4), scales=scales[:], in_=probs_bf[k][:].rearrange("p h x -> p (h x)")
+            )
+            probs_mx[k] = (codes, scales)
+
+        def attend(k):
+            b, gi, ti, last_pass = units[k]
+            v_codes, v_scales = v_mx[b]
+            ctx = ctx_ps_pool.tile([P, H, HD], F32, tag="ctx")
+            for h in range(H):
+                for g in range(G):
+                    codes, scales = probs_mx[k - (G - 1) + g]
+                    nc.tensor.matmul_mx(
+                        out=ctx[:, h, :],
+                        lhsT=codes[:, h * P : (h + 1) * P].bitcast(FP8X4),
+                        lhsT_scale=scales[:, h * P : (h + 1) * P],
+                        rhs=v_codes[:, g, h * HD : (h + 1) * HD].bitcast(FP8X4),
+                        rhs_scale=v_scales[:, g, h * HD : (h + 1) * HD],
+                        start=(g == 0),
+                        stop=(g == G - 1),
+                    )
+            if ti == 0:
+                rows = out_pool.tile([P, H, PACK, HD], F32, tag="rows")
+                staged[(b, gi)] = rows
+            nc.scalar.copy(out=staged[(b, gi)][:, :, ti, :], in_=ctx[:])
+            if ti == PACK - 1:
+                nc.sync.dma_start(
+                    out=out[b].rearrange("(h g m) a -> g m h a", h=H, g=G)[gi],
+                    in_=staged[(b, gi)][:].rearrange("p h t d -> p h (t d)"),
+                )
+
+        load_batch(0)
+        wv_raw = raw_pool.tile([P, PACK, D], BF16, tag="raw_w", bufs=1)
+        nc.sync.dma_start(out=wv_raw[:], in_=Wv.rearrange("(n p) c -> p n c", p=P))
+        nc.sync.dma_start(out=bias_rows[:], in_=bv.partition_broadcast(P))
+        for step in range(TILES):
+            prepare_early(0, step)
+            prepare_late(0, step)
+        load_batch(1)
+        wv_grouped = prep.tile([P, PACK, P, PACK], BF16, tag="grouped", align_bytes=64)
+        for pair in range(2):
+            turn_words(wv_raw, wv_grouped, pair)
+        quantise_grouped(wv_grouped, wv_codes[:], wv_scales[:])
+        for step in range(TILES, UNITS_PER_BATCH):
+            prepare_early(0, step)
+            prepare_late(0, step)
+
+        for r in range(-1, n_units + LAG + 1):
+            b, step = divmod(r, UNITS_PER_BATCH)
+            prepares = 0 <= r < n_units and b + 1 < B
+            if 0 <= r - LAG - 1 < n_units and units[r - LAG - 1][3] == G - 1:
+                attend(r - LAG - 1)
+            if prepares:
+                prepare_early(b + 1, step)
+                if step == TILES and b + 2 < B:
+                    load_batch(b + 2)
+            if 0 <= r - LAG < n_units:
+                normalise(r - LAG)
+            if 0 <= r - 1 < n_units:
+                sum_heads(r - 1)
+            if 0 <= r + 1 < n_units:
+                scores(r + 1)
+                copy_odd_heads(r + 1)
+            if 0 <= r < n_units:
+                subtract_top(r)
+            if r % GROUP == 1 and 0 <= r // GROUP - 1 < n_units // GROUP:
+                reciprocal_of_sums(r // GROUP - 1)
+            if 0 <= r < n_units:
+                exponentials(r)
+            if r % GROUP == 0 and 0 <= r // GROUP - 1 < n_units // GROUP:
+                log_of_sums(r // GROUP - 1)
+            if 0 <= r - LAG < n_units:
+                quantise_probs(r - LAG)
+            if prepares:
+                prepare_late(b + 1, step)

@@ -23,8 +23,9 @@ TILES = G * PACK
 UNIT = P * PACK
 UNITS_PER_BATCH = TILES * G
 GROUP = 4
-LAG = 7
-ODD_FIRST = (1, 3, 0, 2)
+LAG = 6
+ODD_HEADS = (1, 3)
+EVEN_HEADS = (0, 2)
 
 
 def tile_sparseattention_pb_t_kernel(tc, q_rot, k_rot, hidden_states, Wv, bv, out):
@@ -39,12 +40,11 @@ def tile_sparseattention_pb_t_kernel(tc, q_rot, k_rot, hidden_states, Wv, bv, ou
         per_batch = stack.enter_context(tc.tile_pool(name="per_batch", bufs=2))
         soft = stack.enter_context(tc.tile_pool(name="soft", bufs=2))
         exp_pool = stack.enter_context(tc.tile_pool(name="exp", bufs=LAG + 1))
-        sum_pool = stack.enter_context(tc.tile_pool(name="sum", bufs=3))
+        sum_pool = stack.enter_context(tc.tile_pool(name="sum", bufs=LAG))
         code_pool = stack.enter_context(tc.tile_pool(name="codes", bufs=4))
         out_pool = stack.enter_context(tc.tile_pool(name="out", bufs=2))
-        score_ps = stack.enter_context(tc.psum_pool(name="score_ps", bufs=5))
-        ctx_ps_pool = stack.enter_context(tc.psum_pool(name="ctx_ps", bufs=1))
-        prep_ps = stack.enter_context(tc.psum_pool(name="prep_ps", bufs=2))
+        score_ps = stack.enter_context(tc.psum_pool(name="score_ps", bufs=6))
+        other_ps = stack.enter_context(tc.psum_pool(name="other_ps", bufs=2))
         stack.enter_context(tc.manual_schedule())
 
         ident_bf = const.tile([P, P], BF16)
@@ -63,8 +63,10 @@ def tile_sparseattention_pb_t_kernel(tc, q_rot, k_rot, hidden_states, Wv, bv, ou
         grouped_v = {}
         v_mx = {}
         banks = {}
+        pair_tops = {}
         odd_copies = {}
         exps = {}
+        tops = {}
         sums = {}
         probs_bf = {}
         probs_mx = {}
@@ -79,7 +81,7 @@ def tile_sparseattention_pb_t_kernel(tc, q_rot, k_rot, hidden_states, Wv, bv, ou
 
         def turn_words(raw, grouped, pair):
             words = raw[:].bitcast(F32)
-            turned = prep_ps.tile([P, 2, 2, P], F32, tag="prep")
+            turned = other_ps.tile([P, 2, 2, P], F32, tag="other")
             for n in range(2):
                 for u in range(2):
                     nc.tensor.transpose(turned[:, n, u, :], words[:, 2 * pair + n, u * P : (u + 1) * P], ident_f32[:])
@@ -93,7 +95,7 @@ def tile_sparseattention_pb_t_kernel(tc, q_rot, k_rot, hidden_states, Wv, bv, ou
             if tile_index == 0:
                 qk = per_batch.tile([P, G, PACK, 2, H, P], BF16, tag="turned_qk")
                 turned_qk[b] = qk
-            turned = prep_ps.tile([P, 2, H, P], BF16, tag="prep")
+            turned = other_ps.tile([P, 2, H, P], BF16, tag="other")
             for which, name in enumerate(("q", "k")):
                 for h in range(H):
                     nc.tensor.transpose(turned[:, which, h, :], raws[(name, b, g)][:, t, h * HD : (h + 1) * HD], ident_bf[:])
@@ -106,7 +108,7 @@ def tile_sparseattention_pb_t_kernel(tc, q_rot, k_rot, hidden_states, Wv, bv, ou
 
         def project_v(b, g, h):
             codes, scales = hs_mx[b]
-            bank = prep_ps.tile([P, PACK, HD], F32, tag="prep")
+            bank = other_ps.tile([P, PACK, HD], F32, tag="other")
             for t in range(PACK):
                 nc.tensor.matmul_mx(
                     out=bank[:, t, :],
@@ -125,21 +127,14 @@ def tile_sparseattention_pb_t_kernel(tc, q_rot, k_rot, hidden_states, Wv, bv, ou
             if step < 2 * G:
                 g, pair = divmod(step, 2)
                 if pair == 0:
-                    grouped = prep.tile([P, PACK, P, PACK], BF16, tag="grouped", align_bytes=64)
+                    grouped = prep.tile([P, PACK, P, PACK], BF16, tag="grouped", bufs=2, align_bytes=64)
                     grouped_hs[(b, g)] = grouped
                 turn_words(raws[("h", b, g)], grouped_hs[(b, g)], pair)
             if step >= TILES:
                 g, h = divmod(step - TILES, H)
                 project_v(b, g, h)
 
-        def prepare_late(b, step):
-            if step < 2 * G and step % 2 == 1:
-                g = step // 2
-                if g == 0:
-                    hs_codes = prep.tile([P, G, K_PASS], U32, align_bytes=64)
-                    hs_scales = prep.tile([P, G, K_PASS], U8, align_bytes=64)
-                    hs_mx[b] = (hs_codes, hs_scales)
-                quantise_grouped(grouped_hs[(b, g)], hs_mx[b][0][:, g, :], hs_mx[b][1][:, g, :])
+        def prepare_add(b, step):
             if step >= TILES:
                 g, h = divmod(step - TILES, H)
                 if h == 0:
@@ -151,6 +146,17 @@ def tile_sparseattention_pb_t_kernel(tc, q_rot, k_rot, hidden_states, Wv, bv, ou
                     in1=bias_rows[:, h * HD : (h + 1) * HD].unsqueeze(2).to_broadcast([P, HD, PACK]),
                     op=ALU.add,
                 )
+
+        def prepare_quantise(b, step):
+            if step < 2 * G and step % 2 == 1:
+                g = step // 2
+                if g == 0:
+                    hs_codes = prep.tile([P, G, K_PASS], U32, align_bytes=64)
+                    hs_scales = prep.tile([P, G, K_PASS], U8, align_bytes=64)
+                    hs_mx[b] = (hs_codes, hs_scales)
+                quantise_grouped(grouped_hs[(b, g)], hs_mx[b][0][:, g, :], hs_mx[b][1][:, g, :])
+            if step >= TILES:
+                g, h = divmod(step - TILES, H)
                 if h == H - 1:
                     if g == 0:
                         v_codes = per_batch.tile([P, G, A], U32, align_bytes=64)
@@ -158,33 +164,38 @@ def tile_sparseattention_pb_t_kernel(tc, q_rot, k_rot, hidden_states, Wv, bv, ou
                         v_mx[b] = (v_codes, v_scales)
                     quantise_grouped(grouped_v[(b, g)], v_mx[b][0][:, g, :], v_mx[b][1][:, g, :])
 
-        def scores(k):
+        def scores(k, heads):
             b, gi, ti, g = units[k]
             qk = turned_qk[b]
-            banks[k] = {}
-            for h in ODD_FIRST:
+            for h in heads:
                 bank = score_ps.tile([P, P, PACK], F32, tag="scores")
                 for t in range(PACK):
                     nc.tensor.matmul(
                         out=bank[:, :, t], lhsT=qk[:, g, t, 1, h, :], rhs=qk[:, gi, ti, 0, h, :], start=True, stop=True
                     )
-                banks[k][h] = bank[:].rearrange("p i t -> p (i t)")
+                banks[(k, h)] = bank[:].rearrange("p i t -> p (i t)")
 
         def copy_odd_heads(k):
             odd = soft.tile([P, 2, UNIT], BF16, tag="odd")
-            for n in range(2):
-                nc.scalar.copy(out=odd[:, n, :], in_=banks[k][2 * n + 1])
+            for n, h in enumerate(ODD_HEADS):
+                nc.scalar.copy(out=odd[:, n, :], in_=banks[(k, h)])
             odd_copies[k] = odd
 
-        def subtract_top(k):
+        def top_of_pairs(k):
             pair_top = soft.tile([P, 2, UNIT], BF16, tag="pair_top")
-            for n in range(2):
-                nc.vector.tensor_tensor(out=pair_top[:, n, :], in0=banks[k][2 * n], in1=odd_copies[k][:, n, :], op=ALU.max)
+            for n, h in enumerate(EVEN_HEADS):
+                nc.vector.tensor_tensor(out=pair_top[:, n, :], in0=banks[(k, h)], in1=odd_copies[k][:, n, :], op=ALU.max)
+            pair_tops[k] = pair_top
+
+        def top_of_heads(k):
             top = soft.tile([P, UNIT], BF16, tag="top")
-            nc.vector.tensor_tensor(out=top[:], in0=pair_top[:, 0, :], in1=pair_top[:, 1, :], op=ALU.max)
+            nc.vector.tensor_tensor(out=top[:], in0=pair_tops[k][:, 0, :], in1=pair_tops[k][:, 1, :], op=ALU.max)
+            tops[k] = top
+
+        def subtract_top(k):
             shifted = exp_pool.tile([P, H, UNIT], F32, tag="exps")
-            for h in ODD_FIRST:
-                nc.vector.tensor_tensor(out=shifted[:, h, :], in0=banks[k][h], in1=top[:], op=ALU.subtract)
+            for h in ODD_HEADS + EVEN_HEADS:
+                nc.vector.tensor_tensor(out=shifted[:, h, :], in0=banks[(k, h)], in1=tops[k][:], op=ALU.subtract)
             exps[k] = shifted
 
         def exponentials(k):
@@ -192,29 +203,25 @@ def tile_sparseattention_pb_t_kernel(tc, q_rot, k_rot, hidden_states, Wv, bv, ou
             nc.scalar.activation(out=flat, in_=flat, func=ACT.Exp)
 
         def sum_heads(k):
-            group, member = divmod(k, GROUP)
-            if member == 0:
-                total = sum_pool.tile([P, GROUP, UNIT], F32, tag="sums")
-                sums[group] = total
-            half = soft.tile([P, 2, UNIT], F32, tag="half")
-            nc.gpsimd.tensor_tensor(out=half[:], in0=exps[k][:, 0:2, :], in1=exps[k][:, 2:4, :], op=ALU.add)
-            nc.gpsimd.tensor_tensor(out=sums[group][:, member, :], in0=half[:, 0, :], in1=half[:, 1, :], op=ALU.add)
+            total = sum_pool.tile([P, 2, UNIT], F32, tag="sums")
+            nc.gpsimd.tensor_tensor(out=total[:], in0=exps[k][:, 0:2, :], in1=exps[k][:, 2:4, :], op=ALU.add)
+            nc.gpsimd.tensor_tensor(out=total[:, 0, :], in0=total[:, 0, :], in1=total[:, 1, :], op=ALU.add)
+            sums[k] = total
 
         def log_of_sums(group):
-            flat = sums[group][:].rearrange("p m x -> p (m x)")
-            nc.scalar.activation(out=flat, in_=flat, func=ACT.Ln)
+            for k in range(group * GROUP, (group + 1) * GROUP):
+                nc.scalar.activation(out=sums[k][:, 0, :], in_=sums[k][:, 0, :], func=ACT.Ln)
 
         def reciprocal_of_sums(group):
-            flat = sums[group][:].rearrange("p m x -> p (m x)")
-            nc.scalar.activation(out=flat, in_=flat, func=ACT.Exp, scale=-1.0)
+            for k in range(group * GROUP, (group + 1) * GROUP):
+                nc.scalar.activation(out=sums[k][:, 0, :], in_=sums[k][:, 0, :], func=ACT.Exp, scale=-1.0)
 
         def normalise(k):
-            group, member = divmod(k, GROUP)
             probs = soft.tile([P, H, UNIT], BF16, tag="probs", align_bytes=64)
             nc.vector.tensor_tensor(
                 out=probs[:],
                 in0=exps[k][:],
-                in1=sums[group][:, member, :].unsqueeze(1).to_broadcast([P, H, UNIT]),
+                in1=sums[k][:, 0, :].unsqueeze(1).to_broadcast([P, H, UNIT]),
                 op=ALU.mult,
             )
             probs_bf[k] = probs
@@ -230,7 +237,7 @@ def tile_sparseattention_pb_t_kernel(tc, q_rot, k_rot, hidden_states, Wv, bv, ou
         def attend(k):
             b, gi, ti, last_pass = units[k]
             v_codes, v_scales = v_mx[b]
-            ctx = ctx_ps_pool.tile([P, H, HD], F32, tag="ctx")
+            ctx = other_ps.tile([P, H, HD], F32, tag="other")
             for h in range(H):
                 for g in range(G):
                     codes, scales = probs_mx[k - (G - 1) + g]
@@ -259,41 +266,56 @@ def tile_sparseattention_pb_t_kernel(tc, q_rot, k_rot, hidden_states, Wv, bv, ou
         nc.sync.dma_start(out=bias_rows[:], in_=bv.partition_broadcast(P))
         for step in range(TILES):
             prepare_early(0, step)
-            prepare_late(0, step)
+            prepare_add(0, step)
+            prepare_quantise(0, step)
         load_batch(1)
-        wv_grouped = prep.tile([P, PACK, P, PACK], BF16, tag="grouped", align_bytes=64)
+        wv_grouped = prep.tile([P, PACK, P, PACK], BF16, tag="grouped", bufs=2, align_bytes=64)
         for pair in range(2):
             turn_words(wv_raw, wv_grouped, pair)
         quantise_grouped(wv_grouped, wv_codes[:], wv_scales[:])
         for step in range(TILES, UNITS_PER_BATCH):
             prepare_early(0, step)
-            prepare_late(0, step)
+            prepare_add(0, step)
+            prepare_quantise(0, step)
 
-        for r in range(-1, n_units + LAG + 1):
-            b, step = divmod(r, UNITS_PER_BATCH)
-            prepares = 0 <= r < n_units and b + 1 < B
-            if 0 <= r - LAG - 1 < n_units and units[r - LAG - 1][3] == G - 1:
-                attend(r - LAG - 1)
-            if prepares:
-                prepare_early(b + 1, step)
-                if step == TILES and b + 2 < B:
-                    load_batch(b + 2)
-            if 0 <= r - LAG < n_units:
-                normalise(r - LAG)
-            if 0 <= r - 1 < n_units:
-                sum_heads(r - 1)
-            if 0 <= r + 1 < n_units:
-                scores(r + 1)
-                copy_odd_heads(r + 1)
-            if 0 <= r < n_units:
+        def live(k):
+            return 0 <= k < n_units
+
+        for r in range(-2, n_units + LAG + 2):
+            early_b, early_step = divmod(r, UNITS_PER_BATCH)
+            late_b, late_step = divmod(r - 1, UNITS_PER_BATCH)
+            group, member = divmod(r, GROUP)
+            if live(r + 1):
+                scores(r + 1, EVEN_HEADS)
+            if live(r):
                 subtract_top(r)
-            if r % GROUP == 1 and 0 <= r // GROUP - 1 < n_units // GROUP:
-                reciprocal_of_sums(r // GROUP - 1)
-            if 0 <= r < n_units:
+            if live(r + 1):
+                top_of_pairs(r + 1)
+            if live(r - 1) and late_b + 1 < B:
+                prepare_add(late_b + 1, late_step)
+            if live(r + 2):
+                scores(r + 2, ODD_HEADS)
+            if live(r - 1):
+                sum_heads(r - 1)
+            if live(r):
                 exponentials(r)
-            if r % GROUP == 0 and 0 <= r // GROUP - 1 < n_units // GROUP:
-                log_of_sums(r // GROUP - 1)
-            if 0 <= r - LAG < n_units:
-                quantise_probs(r - LAG)
-            if prepares:
-                prepare_late(b + 1, step)
+            if member == 1 and live((group - 1) * GROUP):
+                reciprocal_of_sums(group - 1)
+            if live(r + 2):
+                copy_odd_heads(r + 2)
+            if live(r) and early_b + 1 < B:
+                prepare_early(early_b + 1, early_step)
+                if early_step == TILES and early_b + 2 < B:
+                    load_batch(early_b + 2)
+            if live(r - LAG - 1):
+                quantise_probs(r - LAG - 1)
+                if units[r - LAG - 1][3] == G - 1:
+                    attend(r - LAG - 1)
+            if live(r + 1):
+                top_of_heads(r + 1)
+            if live(r - 1) and late_b + 1 < B:
+                prepare_quantise(late_b + 1, late_step)
+            if live(r - LAG):
+                normalise(r - LAG)
+            if member == 0 and live((group - 1) * GROUP):
+                log_of_sums(group - 1)

@@ -24,6 +24,7 @@ UNIT = P * PACK
 UNITS_PER_BATCH = TILES * G
 GROUP = 4
 LAG = 6
+PREP_LEAD = 10
 ODD_HEADS = (1, 3)
 EVEN_HEADS = (0, 2)
 
@@ -268,22 +269,17 @@ def tile_sparseattention_pb_t_kernel(tc, q_rot, k_rot, hidden_states, Wv, bv, ou
             prepare_early(0, step)
             prepare_add(0, step)
             prepare_quantise(0, step)
-        load_batch(1)
         wv_grouped = prep.tile([P, PACK, P, PACK], BF16, tag="grouped", bufs=2, align_bytes=64)
         for pair in range(2):
             turn_words(wv_raw, wv_grouped, pair)
         quantise_grouped(wv_grouped, wv_codes[:], wv_scales[:])
-        for step in range(TILES, UNITS_PER_BATCH):
-            prepare_early(0, step)
-            prepare_add(0, step)
-            prepare_quantise(0, step)
 
         def live(k):
             return 0 <= k < n_units
 
-        for r in range(-2, n_units + LAG + 2):
-            early_b, early_step = divmod(r, UNITS_PER_BATCH)
-            late_b, late_step = divmod(r - 1, UNITS_PER_BATCH)
+        for r in range(-2, n_units + LAG + 3):
+            early_b, early_step = divmod(r + PREP_LEAD, UNITS_PER_BATCH)
+            late_b, late_step = divmod(r + PREP_LEAD - 1, UNITS_PER_BATCH)
             group, member = divmod(r, GROUP)
             if live(r + 1):
                 scores(r + 1, EVEN_HEADS)
@@ -291,8 +287,8 @@ def tile_sparseattention_pb_t_kernel(tc, q_rot, k_rot, hidden_states, Wv, bv, ou
                 subtract_top(r)
             if live(r + 1):
                 top_of_pairs(r + 1)
-            if live(r - 1) and late_b + 1 < B:
-                prepare_add(late_b + 1, late_step)
+            if late_b < B and r + PREP_LEAD - 1 >= TILES:
+                prepare_add(late_b, late_step)
             if live(r + 2):
                 scores(r + 2, ODD_HEADS)
             if live(r - 1):
@@ -303,19 +299,19 @@ def tile_sparseattention_pb_t_kernel(tc, q_rot, k_rot, hidden_states, Wv, bv, ou
                 reciprocal_of_sums(group - 1)
             if live(r + 2):
                 copy_odd_heads(r + 2)
-            if live(r) and early_b + 1 < B:
-                prepare_early(early_b + 1, early_step)
-                if early_step == TILES and early_b + 2 < B:
-                    load_batch(early_b + 2)
-            if live(r - LAG - 1):
-                quantise_probs(r - LAG - 1)
-                if units[r - LAG - 1][3] == G - 1:
-                    attend(r - LAG - 1)
-            if live(r + 1):
-                top_of_heads(r + 1)
-            if live(r - 1) and late_b + 1 < B:
-                prepare_quantise(late_b + 1, late_step)
+            if early_b < B:
+                prepare_early(early_b, early_step)
+                if early_step == TILES and early_b + 1 < B:
+                    load_batch(early_b + 1)
+            if live(r - LAG - 2) and units[r - LAG - 2][3] == G - 1:
+                attend(r - LAG - 2)
             if live(r - LAG):
                 normalise(r - LAG)
+            if live(r + 1):
+                top_of_heads(r + 1)
+            if late_b < B and r + PREP_LEAD - 1 >= TILES:
+                prepare_quantise(late_b, late_step)
+            if live(r - LAG - 1):
+                quantise_probs(r - LAG - 1)
             if member == 0 and live((group - 1) * GROUP):
                 log_of_sums(group - 1)

@@ -24,14 +24,15 @@ UNIT = P * PACK
 UNITS_PER_BATCH = TILES * G
 GROUP = 4
 LAG = 6
-PREP_LEAD = 10
+PREP_LEAD = 6
+FIRST_ROUND = -2
 ODD_HEADS = (1, 3)
 EVEN_HEADS = (0, 2)
 
 
 def tile_sparseattention_pb_t_kernel(tc, q_rot, k_rot, hidden_states, Wv, bv, out):
     nc = tc.nc
-    units = [(b, gi, ti, g) for b in range(B) for gi in range(G) for ti in range(PACK) for g in range(G)]
+    units = [(b, gi, ti, g) for b in range(B) for gi in range(G) for g in range(G) for ti in range(PACK)]
     n_units = len(units)
 
     with ExitStack() as stack:
@@ -42,8 +43,8 @@ def tile_sparseattention_pb_t_kernel(tc, q_rot, k_rot, hidden_states, Wv, bv, ou
         soft = stack.enter_context(tc.tile_pool(name="soft", bufs=2))
         exp_pool = stack.enter_context(tc.tile_pool(name="exp", bufs=LAG + 1))
         sum_pool = stack.enter_context(tc.tile_pool(name="sum", bufs=LAG))
-        code_pool = stack.enter_context(tc.tile_pool(name="codes", bufs=4))
-        out_pool = stack.enter_context(tc.tile_pool(name="out", bufs=2))
+        code_pool = stack.enter_context(tc.tile_pool(name="codes", bufs=2 * PACK))
+        out_pool = stack.enter_context(tc.tile_pool(name="out", bufs=3))
         score_ps = stack.enter_context(tc.psum_pool(name="score_ps", bufs=6))
         other_ps = stack.enter_context(tc.psum_pool(name="other_ps", bufs=2))
         stack.enter_context(tc.manual_schedule())
@@ -71,7 +72,6 @@ def tile_sparseattention_pb_t_kernel(tc, q_rot, k_rot, hidden_states, Wv, bv, ou
         sums = {}
         probs_bf = {}
         probs_mx = {}
-        staged = {}
 
         def load_batch(b):
             for g in range(G):
@@ -125,8 +125,8 @@ def tile_sparseattention_pb_t_kernel(tc, q_rot, k_rot, hidden_states, Wv, bv, ou
         def prepare_early(b, step):
             if step < TILES:
                 turn_heads(b, step)
-            if step < 2 * G:
-                g, pair = divmod(step, 2)
+            if PACK <= step < TILES:
+                g, pair = divmod(step - PACK, 2)
                 if pair == 0:
                     grouped = prep.tile([P, PACK, P, PACK], BF16, tag="grouped", bufs=2, align_bytes=64)
                     grouped_hs[(b, g)] = grouped
@@ -149,8 +149,8 @@ def tile_sparseattention_pb_t_kernel(tc, q_rot, k_rot, hidden_states, Wv, bv, ou
                 )
 
         def prepare_quantise(b, step):
-            if step < 2 * G and step % 2 == 1:
-                g = step // 2
+            if PACK <= step < TILES and step % 2 == 1:
+                g = (step - PACK) // 2
                 if g == 0:
                     hs_codes = prep.tile([P, G, K_PASS], U32, align_bytes=64)
                     hs_scales = prep.tile([P, G, K_PASS], U8, align_bytes=64)
@@ -241,7 +241,7 @@ def tile_sparseattention_pb_t_kernel(tc, q_rot, k_rot, hidden_states, Wv, bv, ou
             ctx = other_ps.tile([P, H, HD], F32, tag="other")
             for h in range(H):
                 for g in range(G):
-                    codes, scales = probs_mx[k - (G - 1) + g]
+                    codes, scales = probs_mx[k - (G - 1 - g) * PACK]
                     nc.tensor.matmul_mx(
                         out=ctx[:, h, :],
                         lhsT=codes[:, h * P : (h + 1) * P].bitcast(FP8X4),
@@ -251,33 +251,25 @@ def tile_sparseattention_pb_t_kernel(tc, q_rot, k_rot, hidden_states, Wv, bv, ou
                         start=(g == 0),
                         stop=(g == G - 1),
                     )
-            if ti == 0:
-                rows = out_pool.tile([P, H, PACK, HD], F32, tag="rows")
-                staged[(b, gi)] = rows
-            nc.scalar.copy(out=staged[(b, gi)][:, :, ti, :], in_=ctx[:])
-            if ti == PACK - 1:
-                nc.sync.dma_start(
-                    out=out[b].rearrange("(h g m) a -> g m h a", h=H, g=G)[gi],
-                    in_=staged[(b, gi)][:].rearrange("p h t d -> p h (t d)"),
-                )
+            rows = out_pool.tile([P, H, HD], F32, tag="rows")
+            nc.scalar.copy(out=rows[:], in_=ctx[:])
+            nc.sync.dma_start(out=out[b].rearrange("(h g m) (t d) -> g t m h d", h=H, g=G, t=PACK)[gi, ti], in_=rows[:])
 
-        load_batch(0)
         wv_raw = raw_pool.tile([P, PACK, D], BF16, tag="raw_w", bufs=1)
         nc.sync.dma_start(out=wv_raw[:], in_=Wv.rearrange("(n p) c -> p n c", p=P))
+        load_batch(0)
         nc.sync.dma_start(out=bias_rows[:], in_=bv.partition_broadcast(P))
-        for step in range(TILES):
-            prepare_early(0, step)
-            prepare_add(0, step)
-            prepare_quantise(0, step)
         wv_grouped = prep.tile([P, PACK, P, PACK], BF16, tag="grouped", bufs=2, align_bytes=64)
         for pair in range(2):
             turn_words(wv_raw, wv_grouped, pair)
         quantise_grouped(wv_grouped, wv_codes[:], wv_scales[:])
+        for step in range(FIRST_ROUND + PREP_LEAD):
+            prepare_early(0, step)
 
         def live(k):
             return 0 <= k < n_units
 
-        for r in range(-2, n_units + LAG + 3):
+        for r in range(FIRST_ROUND, n_units + LAG + 3):
             early_b, early_step = divmod(r + PREP_LEAD, UNITS_PER_BATCH)
             late_b, late_step = divmod(r + PREP_LEAD - 1, UNITS_PER_BATCH)
             group, member = divmod(r, GROUP)
@@ -287,7 +279,7 @@ def tile_sparseattention_pb_t_kernel(tc, q_rot, k_rot, hidden_states, Wv, bv, ou
                 subtract_top(r)
             if live(r + 1):
                 top_of_pairs(r + 1)
-            if late_b < B and r + PREP_LEAD - 1 >= TILES:
+            if late_b < B:
                 prepare_add(late_b, late_step)
             if live(r + 2):
                 scores(r + 2, ODD_HEADS)
@@ -309,7 +301,7 @@ def tile_sparseattention_pb_t_kernel(tc, q_rot, k_rot, hidden_states, Wv, bv, ou
                 normalise(r - LAG)
             if live(r + 1):
                 top_of_heads(r + 1)
-            if late_b < B and r + PREP_LEAD - 1 >= TILES:
+            if late_b < B:
                 prepare_quantise(late_b, late_step)
             if live(r - LAG - 1):
                 quantise_probs(r - LAG - 1)

@@ -22,12 +22,18 @@ G = S // K_PASS
 TILES = G * PACK
 UNIT = P * PACK
 UNITS_PER_BATCH = TILES * G
-GROUP = 4
-LAG = 6
+GROUP = 6
+LAG = GROUP + 3
 PREP_LEAD = 6
+HEAD_STEPS = TILES
+WORD_STEP = 4
+V_STEP = TILES
+PREP_STEPS = V_STEP + G * H
 FIRST_ROUND = -2
-ODD_HEADS = (1, 3)
 EVEN_HEADS = (0, 2)
+ODD_HEADS = (1, 3)
+SLOT = {0: 0, 2: 1, 1: 2, 3: 3}
+QK_AHEAD = 4
 
 
 def tile_sparseattention_pb_t_kernel(tc, q_rot, k_rot, hidden_states, Wv, bv, out):
@@ -37,15 +43,19 @@ def tile_sparseattention_pb_t_kernel(tc, q_rot, k_rot, hidden_states, Wv, bv, ou
 
     with ExitStack() as stack:
         const = stack.enter_context(tc.tile_pool(name="const", bufs=1))
-        raw_pool = stack.enter_context(tc.tile_pool(name="raw", bufs=G))
+        raw_pool = stack.enter_context(tc.tile_pool(name="raw", bufs=QK_AHEAD))
         prep = stack.enter_context(tc.tile_pool(name="prep", bufs=1))
         per_batch = stack.enter_context(tc.tile_pool(name="per_batch", bufs=2))
         soft = stack.enter_context(tc.tile_pool(name="soft", bufs=2))
+        copy_pool = stack.enter_context(tc.tile_pool(name="copies", bufs=3))
         exp_pool = stack.enter_context(tc.tile_pool(name="exp", bufs=LAG + 1))
-        sum_pool = stack.enter_context(tc.tile_pool(name="sum", bufs=LAG))
-        code_pool = stack.enter_context(tc.tile_pool(name="codes", bufs=2 * PACK))
-        out_pool = stack.enter_context(tc.tile_pool(name="out", bufs=3))
-        score_ps = stack.enter_context(tc.psum_pool(name="score_ps", bufs=6))
+        sum_pool = stack.enter_context(tc.tile_pool(name="sum", bufs=LAG + 1))
+        code_pool = stack.enter_context(tc.tile_pool(name="codes", bufs=PACK + 2))
+        out_pool = stack.enter_context(tc.tile_pool(name="out", bufs=2))
+        even_ps = stack.enter_context(tc.psum_pool(name="even_ps", bufs=2))
+        odd_ps = stack.enter_context(tc.psum_pool(name="odd_ps", bufs=2))
+        sum_ps = stack.enter_context(tc.psum_pool(name="sum_ps", bufs=1))
+        factor_ps = stack.enter_context(tc.psum_pool(name="factor_ps", bufs=1))
         other_ps = stack.enter_context(tc.psum_pool(name="other_ps", bufs=2))
         stack.enter_context(tc.manual_schedule())
 
@@ -57,7 +67,8 @@ def tile_sparseattention_pb_t_kernel(tc, q_rot, k_rot, hidden_states, Wv, bv, ou
         wv_codes = const.tile([P, A], U32, align_bytes=64)
         wv_scales = const.tile([P, A], U8, align_bytes=64)
 
-        raws = {}
+        qk_raws = {}
+        h_raws = {}
         turned_qk = {}
         hs_mx = {}
         grouped_hs = {}
@@ -65,20 +76,34 @@ def tile_sparseattention_pb_t_kernel(tc, q_rot, k_rot, hidden_states, Wv, bv, ou
         grouped_v = {}
         v_mx = {}
         banks = {}
-        pair_tops = {}
         odd_copies = {}
-        exps = {}
+        pair_tops = {}
         tops = {}
-        sums = {}
+        exps = {}
+        sum_banks = {}
+        factors = {}
+        factor_banks = {}
         probs_bf = {}
         probs_mx = {}
+        ctx_banks = {}
 
-        def load_batch(b):
-            for g in range(G):
-                for name, x in (("k", k_rot), ("q", q_rot), ("h", hidden_states)):
-                    raw = raw_pool.tile([P, PACK, D], BF16, tag="raw_" + name, name="raw_" + name)
-                    nc.sync.dma_start(out=raw[:], in_=x[b].rearrange("(g p t) c -> g p t c", g=G, p=P)[g])
-                    raws[(name, b, g)] = raw
+        def load_qk(n):
+            b, tile_index = divmod(n, TILES)
+            if b < B:
+                g, t = divmod(tile_index, PACK)
+                pair = []
+                for name, x in (("k", k_rot), ("q", q_rot)):
+                    raw = raw_pool.tile([P, D], BF16, tag="raw_" + name, name="raw_" + name)
+                    nc.sync.dma_start(out=raw[:], in_=x[b].rearrange("(g p t) c -> g t p c", g=G, p=P)[g, t])
+                    pair.append(raw)
+                qk_raws[(b, tile_index)] = pair
+
+        def load_hidden(b):
+            if b < B:
+                for g in range(G):
+                    raw = raw_pool.tile([P, PACK, D], BF16, tag="raw_h", name="raw_h", bufs=G)
+                    nc.sync.dma_start(out=raw[:], in_=hidden_states[b].rearrange("(g p t) c -> g p t c", g=G, p=P)[g])
+                    h_raws[(b, g)] = raw
 
         def turn_words(raw, grouped, pair):
             words = raw[:].bitcast(F32)
@@ -96,11 +121,13 @@ def tile_sparseattention_pb_t_kernel(tc, q_rot, k_rot, hidden_states, Wv, bv, ou
             if tile_index == 0:
                 qk = per_batch.tile([P, G, PACK, 2, H, P], BF16, tag="turned_qk")
                 turned_qk[b] = qk
+            k_raw, q_raw = qk_raws[(b, tile_index)]
             turned = other_ps.tile([P, 2, H, P], BF16, tag="other")
-            for which, name in enumerate(("q", "k")):
+            for which, raw in enumerate((q_raw, k_raw)):
                 for h in range(H):
-                    nc.tensor.transpose(turned[:, which, h, :], raws[(name, b, g)][:, t, h * HD : (h + 1) * HD], ident_bf[:])
+                    nc.tensor.transpose(turned[:, which, h, :], raw[:, h * HD : (h + 1) * HD], ident_bf[:])
             nc.scalar.copy(out=turned_qk[b][:, g, t, :, :, :], in_=turned[:])
+            load_qk(b * TILES + tile_index + QK_AHEAD)
 
         def quantise_grouped(grouped, codes, scales):
             nc.vector.quantize_mx(
@@ -122,22 +149,26 @@ def tile_sparseattention_pb_t_kernel(tc, q_rot, k_rot, hidden_states, Wv, bv, ou
                 )
             v_banks[(b, g, h)] = bank
 
-        def prepare_early(b, step):
-            if step < TILES:
+        def prepare_turns(b, step):
+            if step < HEAD_STEPS:
                 turn_heads(b, step)
-            if PACK <= step < TILES:
-                g, pair = divmod(step - PACK, 2)
+            if WORD_STEP <= step < WORD_STEP + 2 * G:
+                g, pair = divmod(step - WORD_STEP, 2)
                 if pair == 0:
                     grouped = prep.tile([P, PACK, P, PACK], BF16, tag="grouped", bufs=2, align_bytes=64)
                     grouped_hs[(b, g)] = grouped
-                turn_words(raws[("h", b, g)], grouped_hs[(b, g)], pair)
-            if step >= TILES:
-                g, h = divmod(step - TILES, H)
+                turn_words(h_raws[(b, g)], grouped_hs[(b, g)], pair)
+                if step == WORD_STEP + 2 * G - 1:
+                    load_hidden(b + 1)
+
+        def prepare_project(b, step):
+            if step >= V_STEP:
+                g, h = divmod(step - V_STEP, H)
                 project_v(b, g, h)
 
         def prepare_add(b, step):
-            if step >= TILES:
-                g, h = divmod(step - TILES, H)
+            if step >= V_STEP:
+                g, h = divmod(step - V_STEP, H)
                 if h == 0:
                     grouped = prep.tile([P, H, HD, PACK], BF16, tag="grouped_v", align_bytes=64)
                     grouped_v[(b, g)] = grouped
@@ -149,15 +180,15 @@ def tile_sparseattention_pb_t_kernel(tc, q_rot, k_rot, hidden_states, Wv, bv, ou
                 )
 
         def prepare_quantise(b, step):
-            if PACK <= step < TILES and step % 2 == 1:
-                g = (step - PACK) // 2
+            if WORD_STEP <= step < WORD_STEP + 2 * G and (step - WORD_STEP) % 2 == 1:
+                g = (step - WORD_STEP) // 2
                 if g == 0:
                     hs_codes = prep.tile([P, G, K_PASS], U32, align_bytes=64)
                     hs_scales = prep.tile([P, G, K_PASS], U8, align_bytes=64)
                     hs_mx[b] = (hs_codes, hs_scales)
                 quantise_grouped(grouped_hs[(b, g)], hs_mx[b][0][:, g, :], hs_mx[b][1][:, g, :])
-            if step >= TILES:
-                g, h = divmod(step - TILES, H)
+            if step >= V_STEP:
+                g, h = divmod(step - V_STEP, H)
                 if h == H - 1:
                     if g == 0:
                         v_codes = per_batch.tile([P, G, A], U32, align_bytes=64)
@@ -165,67 +196,89 @@ def tile_sparseattention_pb_t_kernel(tc, q_rot, k_rot, hidden_states, Wv, bv, ou
                         v_mx[b] = (v_codes, v_scales)
                     quantise_grouped(grouped_v[(b, g)], v_mx[b][0][:, g, :], v_mx[b][1][:, g, :])
 
-        def scores(k, heads):
+        def scores(k, heads, pool):
             b, gi, ti, g = units[k]
             qk = turned_qk[b]
             for h in heads:
-                bank = score_ps.tile([P, P, PACK], F32, tag="scores")
+                bank = pool.tile([P, PACK, P], F32, tag="scores")
                 for t in range(PACK):
                     nc.tensor.matmul(
-                        out=bank[:, :, t], lhsT=qk[:, g, t, 1, h, :], rhs=qk[:, gi, ti, 0, h, :], start=True, stop=True
+                        out=bank[:, t, :], lhsT=qk[:, g, t, 1, h, :], rhs=qk[:, gi, ti, 0, h, :], start=True, stop=True
                     )
-                banks[(k, h)] = bank[:].rearrange("p i t -> p (i t)")
+                banks[(k, h)] = bank[:].rearrange("p t i -> p i t")
 
         def copy_odd_heads(k):
-            odd = soft.tile([P, 2, UNIT], BF16, tag="odd")
+            odd = copy_pool.tile([P, 2, P, PACK], F32, tag="odd")
             for n, h in enumerate(ODD_HEADS):
-                nc.scalar.copy(out=odd[:, n, :], in_=banks[(k, h)])
+                nc.scalar.copy(out=odd[:, n, :, :], in_=banks[(k, h)])
             odd_copies[k] = odd
 
         def top_of_pairs(k):
-            pair_top = soft.tile([P, 2, UNIT], BF16, tag="pair_top")
+            pair_top = soft.tile([P, 2, P, PACK], BF16, tag="pair_top")
             for n, h in enumerate(EVEN_HEADS):
-                nc.vector.tensor_tensor(out=pair_top[:, n, :], in0=banks[(k, h)], in1=odd_copies[k][:, n, :], op=ALU.max)
+                nc.vector.tensor_tensor(
+                    out=pair_top[:, n, :, :], in0=banks[(k, h)], in1=odd_copies[k][:, n, :, :], op=ALU.max
+                )
             pair_tops[k] = pair_top
 
         def top_of_heads(k):
-            top = soft.tile([P, UNIT], BF16, tag="top")
-            nc.vector.tensor_tensor(out=top[:], in0=pair_tops[k][:, 0, :], in1=pair_tops[k][:, 1, :], op=ALU.max)
+            top = soft.tile([P, P, PACK], BF16, tag="top")
+            nc.vector.tensor_tensor(out=top[:], in0=pair_tops[k][:, 0, :, :], in1=pair_tops[k][:, 1, :, :], op=ALU.max)
             tops[k] = top
 
         def subtract_top(k):
-            shifted = exp_pool.tile([P, H, UNIT], F32, tag="exps")
-            for h in ODD_HEADS + EVEN_HEADS:
-                nc.vector.tensor_tensor(out=shifted[:, h, :], in0=banks[(k, h)], in1=tops[k][:], op=ALU.subtract)
-            exps[k] = shifted
+            shifted = exp_pool.tile([P, H, P, PACK], F32, tag="exps")
+            for h in EVEN_HEADS:
+                nc.vector.tensor_tensor(out=shifted[:, SLOT[h], :, :], in0=banks[(k, h)], in1=tops[k][:], op=ALU.subtract)
+            for n, h in enumerate(ODD_HEADS):
+                nc.gpsimd.tensor_tensor(
+                    out=shifted[:, SLOT[h], :, :], in0=odd_copies[k][:, n, :, :], in1=tops[k][:], op=ALU.subtract
+                )
+            exps[k] = shifted[:].rearrange("p h i t -> p h (i t)")
 
         def exponentials(k):
-            flat = exps[k][:].rearrange("p h x -> p (h x)")
-            nc.scalar.activation(out=flat, in_=flat, func=ACT.Exp)
+            for n in range(2):
+                part = exps[k][:, 2 * n : 2 * n + 2, :]
+                nc.scalar.activation(out=part, in_=part, func=ACT.Exp)
 
         def sum_heads(k):
-            total = sum_pool.tile([P, 2, UNIT], F32, tag="sums")
-            nc.gpsimd.tensor_tensor(out=total[:], in0=exps[k][:, 0:2, :], in1=exps[k][:, 2:4, :], op=ALU.add)
-            nc.gpsimd.tensor_tensor(out=total[:, 0, :], in0=total[:, 0, :], in1=total[:, 1, :], op=ALU.add)
-            sums[k] = total
+            bank = sum_ps.tile([P, PACK, P], F32, tag="sum")
+            for c in range(PACK):
+                for n in range(H):
+                    nc.tensor.matmul(
+                        out=bank[:, c, :],
+                        lhsT=exps[k][:, n, c * P : (c + 1) * P],
+                        rhs=ident_f32[:],
+                        start=(n == 0),
+                        stop=(n == H - 1),
+                        is_transpose=True,
+                    )
+            sum_banks[k] = bank
 
-        def log_of_sums(group):
-            for k in range(group * GROUP, (group + 1) * GROUP):
-                nc.scalar.activation(out=sums[k][:, 0, :], in_=sums[k][:, 0, :], func=ACT.Ln)
+        def square_sum(k):
+            square = sum_pool.tile([P, PACK, P], F32, tag="square")
+            nc.scalar.activation(out=square[:], in_=sum_banks[k][:], func=ACT.Square)
+            factors[k] = square
 
-        def reciprocal_of_sums(group):
-            for k in range(group * GROUP, (group + 1) * GROUP):
-                nc.scalar.activation(out=sums[k][:, 0, :], in_=sums[k][:, 0, :], func=ACT.Exp, scale=-1.0)
+        def reciprocal_of_sum(k):
+            nc.scalar.activation(out=factors[k][:], in_=factors[k][:], func=ACT.Abs_reciprocal_sqrt)
 
-        def normalise(k):
-            probs = soft.tile([P, H, UNIT], BF16, tag="probs", align_bytes=64)
+        def turn_factor(k):
+            bank = factor_ps.tile([P, UNIT], F32, tag="factor")
+            for c in range(PACK):
+                nc.tensor.transpose(bank[:, c * P : (c + 1) * P], factors[k][:, c, :], ident_f32[:])
+            factor_banks[k] = bank
+
+        def normalise(k, first, last):
+            if first == 0:
+                probs = soft.tile([P, H, UNIT], BF16, tag="probs", align_bytes=64)
+                probs_bf[k] = probs
             nc.vector.tensor_tensor(
-                out=probs[:],
-                in0=exps[k][:],
-                in1=sums[k][:, 0, :].unsqueeze(1).to_broadcast([P, H, UNIT]),
+                out=probs_bf[k][:, first:last, :],
+                in0=exps[k][:, first:last, :],
+                in1=factor_banks[k][:].unsqueeze(1).to_broadcast([P, last - first, UNIT]),
                 op=ALU.mult,
             )
-            probs_bf[k] = probs
 
         def quantise_probs(k):
             codes = code_pool.tile([P, H * P], U32, tag="probs_codes", align_bytes=64)
@@ -236,74 +289,92 @@ def tile_sparseattention_pb_t_kernel(tc, q_rot, k_rot, hidden_states, Wv, bv, ou
             probs_mx[k] = (codes, scales)
 
         def attend(k):
-            b, gi, ti, last_pass = units[k]
-            v_codes, v_scales = v_mx[b]
+            v_codes, v_scales = v_mx[units[k][0]]
             ctx = other_ps.tile([P, H, HD], F32, tag="other")
             for h in range(H):
+                n = SLOT[h]
                 for g in range(G):
                     codes, scales = probs_mx[k - (G - 1 - g) * PACK]
                     nc.tensor.matmul_mx(
                         out=ctx[:, h, :],
-                        lhsT=codes[:, h * P : (h + 1) * P].bitcast(FP8X4),
-                        lhsT_scale=scales[:, h * P : (h + 1) * P],
+                        lhsT=codes[:, n * P : (n + 1) * P].bitcast(FP8X4),
+                        lhsT_scale=scales[:, n * P : (n + 1) * P],
                         rhs=v_codes[:, g, h * HD : (h + 1) * HD].bitcast(FP8X4),
                         rhs_scale=v_scales[:, g, h * HD : (h + 1) * HD],
                         start=(g == 0),
                         stop=(g == G - 1),
                     )
+            ctx_banks[k] = ctx
+
+        def store_ctx(k):
+            b, gi, ti, last_pass = units[k]
             rows = out_pool.tile([P, H, HD], F32, tag="rows")
-            nc.scalar.copy(out=rows[:], in_=ctx[:])
+            nc.scalar.copy(out=rows[:], in_=ctx_banks[k][:])
             nc.sync.dma_start(out=out[b].rearrange("(h g m) (t d) -> g t m h d", h=H, g=G, t=PACK)[gi, ti], in_=rows[:])
 
-        wv_raw = raw_pool.tile([P, PACK, D], BF16, tag="raw_w", bufs=1)
+        wv_raw = prep.tile([P, PACK, D], BF16, tag="grouped_v", align_bytes=64)
         nc.sync.dma_start(out=wv_raw[:], in_=Wv.rearrange("(n p) c -> p n c", p=P))
-        load_batch(0)
+        for n in range(QK_AHEAD):
+            load_qk(n)
+        load_hidden(0)
         nc.sync.dma_start(out=bias_rows[:], in_=bv.partition_broadcast(P))
         wv_grouped = prep.tile([P, PACK, P, PACK], BF16, tag="grouped", bufs=2, align_bytes=64)
         for pair in range(2):
             turn_words(wv_raw, wv_grouped, pair)
         quantise_grouped(wv_grouped, wv_codes[:], wv_scales[:])
         for step in range(FIRST_ROUND + PREP_LEAD):
-            prepare_early(0, step)
+            prepare_turns(0, step)
 
         def live(k):
             return 0 <= k < n_units
 
+        def prep_at(r):
+            b, step = divmod(r + PREP_LEAD, UNITS_PER_BATCH)
+            return b, step, b < B
+
         for r in range(FIRST_ROUND, n_units + LAG + 3):
-            early_b, early_step = divmod(r + PREP_LEAD, UNITS_PER_BATCH)
-            late_b, late_step = divmod(r + PREP_LEAD - 1, UNITS_PER_BATCH)
-            group, member = divmod(r, GROUP)
-            if live(r + 1):
-                scores(r + 1, EVEN_HEADS)
+            now_b, now_step, now_live = prep_at(r)
+            old_b, old_step, old_live = prep_at(r - 1)
+            k = r - LAG
+            if live(r + 2):
+                scores(r + 2, ODD_HEADS, odd_ps)
+            if live(k):
+                normalise(k, 0, 1)
             if live(r):
                 subtract_top(r)
-            if live(r + 1):
-                top_of_pairs(r + 1)
-            if late_b < B:
-                prepare_add(late_b, late_step)
-            if live(r + 2):
-                scores(r + 2, ODD_HEADS)
-            if live(r - 1):
-                sum_heads(r - 1)
-            if live(r):
-                exponentials(r)
-            if member == 1 and live((group - 1) * GROUP):
-                reciprocal_of_sums(group - 1)
+            if live(k - 2) and units[k - 2][3] == G - 1:
+                store_ctx(k - 2)
             if live(r + 2):
                 copy_odd_heads(r + 2)
-            if early_b < B:
-                prepare_early(early_b, early_step)
-                if early_step == TILES and early_b + 1 < B:
-                    load_batch(early_b + 1)
-            if live(r - LAG - 2) and units[r - LAG - 2][3] == G - 1:
-                attend(r - LAG - 2)
-            if live(r - LAG):
-                normalise(r - LAG)
+            if live(r - 2):
+                square_sum(r - 2)
+            if live(r):
+                exponentials(r)
+            if live(r + 1):
+                scores(r + 1, EVEN_HEADS, even_ps)
+            if now_live:
+                prepare_turns(now_b, now_step)
+            if live(k):
+                normalise(k, 1, H)
+            if live(r + 1):
+                top_of_pairs(r + 1)
+            if old_live:
+                prepare_add(old_b, old_step)
+            if live(k):
+                quantise_probs(k)
+            if old_live:
+                prepare_quantise(old_b, old_step)
             if live(r + 1):
                 top_of_heads(r + 1)
-            if late_b < B:
-                prepare_quantise(late_b, late_step)
-            if live(r - LAG - 1):
-                quantise_probs(r - LAG - 1)
-            if member == 0 and live((group - 1) * GROUP):
-                log_of_sums(group - 1)
+            if live(k + 1):
+                turn_factor(k + 1)
+            if live(r - 1):
+                sum_heads(r - 1)
+            if now_live:
+                prepare_project(now_b, now_step)
+            if live(k - 1) and units[k - 1][3] == G - 1:
+                attend(k - 1)
+            last = r - 2
+            if live(last) and (last % GROUP == GROUP - 1 or last == n_units - 1):
+                for member in range(last - last % GROUP, last + 1):
+                    reciprocal_of_sum(member)

@@ -48,6 +48,7 @@ def tile_sparseattention_pb_t_kernel(tc, q_rot, k_rot, hidden_states, Wv, bv, ou
         per_batch = stack.enter_context(tc.tile_pool(name="per_batch", bufs=2))
         soft = stack.enter_context(tc.tile_pool(name="soft", bufs=2))
         copy_pool = stack.enter_context(tc.tile_pool(name="copies", bufs=3))
+        pair_pool = stack.enter_context(tc.tile_pool(name="pairs", bufs=2))
         exp_pool = stack.enter_context(tc.tile_pool(name="exp", bufs=LAG + 1))
         sum_pool = stack.enter_context(tc.tile_pool(name="sum", bufs=LAG + 1))
         code_pool = stack.enter_context(tc.tile_pool(name="codes", bufs=PACK + 2))
@@ -80,6 +81,7 @@ def tile_sparseattention_pb_t_kernel(tc, q_rot, k_rot, hidden_states, Wv, bv, ou
         pair_tops = {}
         tops = {}
         exps = {}
+        pair_sums = {}
         sum_banks = {}
         factors = {}
         factor_banks = {}
@@ -236,21 +238,26 @@ def tile_sparseattention_pb_t_kernel(tc, q_rot, k_rot, hidden_states, Wv, bv, ou
                 )
             exps[k] = shifted[:].rearrange("p h i t -> p h (i t)")
 
-        def exponentials(k):
-            for n in range(2):
-                part = exps[k][:, 2 * n : 2 * n + 2, :]
-                nc.scalar.activation(out=part, in_=part, func=ACT.Exp)
+        def exponentials(k, first, last):
+            part = exps[k][:, first:last, :]
+            nc.scalar.activation(out=part, in_=part, func=ACT.Exp)
+
+        def add_pair(k):
+            pair = pair_pool.tile([P, UNIT], F32, tag="pair")
+            nc.gpsimd.tensor_tensor(out=pair[:], in0=exps[k][:, 0, :], in1=exps[k][:, 1, :], op=ALU.add)
+            pair_sums[k] = pair
 
         def sum_heads(k):
+            parts = (pair_sums[k][:], exps[k][:, 2, :], exps[k][:, 3, :])
             bank = sum_ps.tile([P, PACK, P], F32, tag="sum")
             for c in range(PACK):
-                for n in range(H):
+                for n, part in enumerate(parts):
                     nc.tensor.matmul(
                         out=bank[:, c, :],
-                        lhsT=exps[k][:, n, c * P : (c + 1) * P],
+                        lhsT=part[:, c * P : (c + 1) * P],
                         rhs=ident_f32[:],
                         start=(n == 0),
-                        stop=(n == H - 1),
+                        stop=(n == len(parts) - 1),
                         is_transpose=True,
                     )
             sum_banks[k] = bank
@@ -312,16 +319,12 @@ def tile_sparseattention_pb_t_kernel(tc, q_rot, k_rot, hidden_states, Wv, bv, ou
             nc.scalar.copy(out=rows[:], in_=ctx_banks[k][:])
             nc.sync.dma_start(out=out[b].rearrange("(h g m) (t d) -> g t m h d", h=H, g=G, t=PACK)[gi, ti], in_=rows[:])
 
-        wv_raw = prep.tile([P, PACK, D], BF16, tag="grouped_v", align_bytes=64)
-        nc.sync.dma_start(out=wv_raw[:], in_=Wv.rearrange("(n p) c -> p n c", p=P))
         for n in range(QK_AHEAD):
             load_qk(n)
+        wv_raw = prep.tile([P, PACK, D], BF16, tag="grouped_v", align_bytes=64)
+        nc.sync.dma_start(out=wv_raw[:], in_=Wv.rearrange("(n p) c -> p n c", p=P))
         load_hidden(0)
         nc.sync.dma_start(out=bias_rows[:], in_=bv.partition_broadcast(P))
-        wv_grouped = prep.tile([P, PACK, P, PACK], BF16, tag="grouped", bufs=2, align_bytes=64)
-        for pair in range(2):
-            turn_words(wv_raw, wv_grouped, pair)
-        quantise_grouped(wv_grouped, wv_codes[:], wv_scales[:])
         for step in range(FIRST_ROUND + PREP_LEAD):
             prepare_turns(0, step)
 
@@ -338,10 +341,16 @@ def tile_sparseattention_pb_t_kernel(tc, q_rot, k_rot, hidden_states, Wv, bv, ou
             k = r - LAG
             if live(r + 2):
                 scores(r + 2, ODD_HEADS, odd_ps)
+            if r == FIRST_ROUND + 1:
+                wv_grouped = prep.tile([P, PACK, P, PACK], BF16, tag="grouped_w", align_bytes=64)
+                for pair in range(2):
+                    turn_words(wv_raw, wv_grouped, pair)
             if live(k):
                 normalise(k, 0, 1)
             if live(r):
                 subtract_top(r)
+            if live(r - 1):
+                add_pair(r - 1)
             if live(k - 2) and units[k - 2][3] == G - 1:
                 store_ctx(k - 2)
             if live(r + 2):
@@ -349,11 +358,13 @@ def tile_sparseattention_pb_t_kernel(tc, q_rot, k_rot, hidden_states, Wv, bv, ou
             if live(r - 2):
                 square_sum(r - 2)
             if live(r):
-                exponentials(r)
+                exponentials(r, 0, 2)
             if live(r + 1):
                 scores(r + 1, EVEN_HEADS, even_ps)
             if now_live:
                 prepare_turns(now_b, now_step)
+            if live(r):
+                exponentials(r, 2, 4)
             if live(k):
                 normalise(k, 1, H)
             if live(r + 1):
@@ -362,6 +373,8 @@ def tile_sparseattention_pb_t_kernel(tc, q_rot, k_rot, hidden_states, Wv, bv, ou
                 prepare_add(old_b, old_step)
             if live(k):
                 quantise_probs(k)
+            if r == FIRST_ROUND + 2:
+                quantise_grouped(wv_grouped, wv_codes[:], wv_scales[:])
             if old_live:
                 prepare_quantise(old_b, old_step)
             if live(r + 1):

@@ -22,7 +22,7 @@ G = S // K_PASS
 TILES = G * PACK
 UNIT = P * PACK
 UNITS_PER_BATCH = TILES * G
-GROUP = 6
+GROUP = 4
 LAG = GROUP + 3
 PREP_LEAD = 6
 HEAD_STEPS = TILES
@@ -209,19 +209,19 @@ def tile_sparseattention_pb_t_kernel(tc, q_rot, k_rot, hidden_states, Wv, bv, ou
                     )
                 banks[(k, h)] = bank[:].rearrange("p t i -> p i t")
 
-        def copy_odd_heads(k):
-            odd = copy_pool.tile([P, 2, P, PACK], F32, tag="odd")
-            for n, h in enumerate(ODD_HEADS):
-                nc.scalar.copy(out=odd[:, n, :, :], in_=banks[(k, h)])
-            odd_copies[k] = odd
+        def copy_odd_head(k, n):
+            if n == 0:
+                odd = copy_pool.tile([P, 2, P, PACK], F32, tag="odd")
+                odd_copies[k] = odd
+            nc.scalar.copy(out=odd_copies[k][:, n, :, :], in_=banks[(k, ODD_HEADS[n])])
 
-        def top_of_pairs(k):
-            pair_top = soft.tile([P, 2, P, PACK], BF16, tag="pair_top")
-            for n, h in enumerate(EVEN_HEADS):
-                nc.vector.tensor_tensor(
-                    out=pair_top[:, n, :, :], in0=banks[(k, h)], in1=odd_copies[k][:, n, :, :], op=ALU.max
-                )
-            pair_tops[k] = pair_top
+        def top_of_pair(k, n):
+            if n == 0:
+                pair_top = soft.tile([P, 2, P, PACK], BF16, tag="pair_top")
+                pair_tops[k] = pair_top
+            nc.vector.tensor_tensor(
+                out=pair_tops[k][:, n, :, :], in0=banks[(k, EVEN_HEADS[n])], in1=odd_copies[k][:, n, :, :], op=ALU.max
+            )
 
         def top_of_heads(k):
             top = soft.tile([P, P, PACK], BF16, tag="top")
@@ -276,16 +276,15 @@ def tile_sparseattention_pb_t_kernel(tc, q_rot, k_rot, hidden_states, Wv, bv, ou
                 nc.tensor.transpose(bank[:, c * P : (c + 1) * P], factors[k][:, c, :], ident_f32[:])
             factor_banks[k] = bank
 
-        def normalise(k, first, last):
-            if first == 0:
-                probs = soft.tile([P, H, UNIT], BF16, tag="probs", align_bytes=64)
-                probs_bf[k] = probs
+        def normalise(k):
+            probs = soft.tile([P, H, UNIT], BF16, tag="probs", align_bytes=64)
             nc.vector.tensor_tensor(
-                out=probs_bf[k][:, first:last, :],
-                in0=exps[k][:, first:last, :],
-                in1=factor_banks[k][:].unsqueeze(1).to_broadcast([P, last - first, UNIT]),
+                out=probs[:],
+                in0=exps[k][:],
+                in1=factor_banks[k][:].unsqueeze(1).to_broadcast([P, H, UNIT]),
                 op=ALU.mult,
             )
+            probs_bf[k] = probs
 
         def quantise_probs(k):
             codes = code_pool.tile([P, H * P], U32, tag="probs_codes", align_bytes=64)
@@ -345,8 +344,8 @@ def tile_sparseattention_pb_t_kernel(tc, q_rot, k_rot, hidden_states, Wv, bv, ou
                 wv_grouped = prep.tile([P, PACK, P, PACK], BF16, tag="grouped_w", align_bytes=64)
                 for pair in range(2):
                     turn_words(wv_raw, wv_grouped, pair)
-            if live(k):
-                normalise(k, 0, 1)
+            if live(k - 1):
+                quantise_probs(k - 1)
             if live(r):
                 subtract_top(r)
             if live(r - 1):
@@ -354,7 +353,8 @@ def tile_sparseattention_pb_t_kernel(tc, q_rot, k_rot, hidden_states, Wv, bv, ou
             if live(k - 2) and units[k - 2][3] == G - 1:
                 store_ctx(k - 2)
             if live(r + 2):
-                copy_odd_heads(r + 2)
+                copy_odd_head(r + 2, 0)
+                copy_odd_head(r + 2, 1)
             if live(r - 2):
                 square_sum(r - 2)
             if live(r):
@@ -366,13 +366,12 @@ def tile_sparseattention_pb_t_kernel(tc, q_rot, k_rot, hidden_states, Wv, bv, ou
             if live(r):
                 exponentials(r, 2, 4)
             if live(k):
-                normalise(k, 1, H)
+                normalise(k)
             if live(r + 1):
-                top_of_pairs(r + 1)
+                top_of_pair(r + 1, 0)
+                top_of_pair(r + 1, 1)
             if old_live:
                 prepare_add(old_b, old_step)
-            if live(k):
-                quantise_probs(k)
             if r == FIRST_ROUND + 2:
                 quantise_grouped(wv_grouped, wv_codes[:], wv_scales[:])
             if old_live:

@@ -23,7 +23,7 @@ TILES = G * PACK
 UNIT = P * PACK
 UNITS_PER_BATCH = TILES * G
 GROUP = 4
-LAG = GROUP + 3
+LAG = GROUP + 4
 PREP_LEAD = 6
 HEAD_STEPS = TILES
 WORD_STEP = 4
@@ -344,25 +344,30 @@ def tile_sparseattention_pb_t_kernel(tc, q_rot, k_rot, hidden_states, Wv, bv, ou
                 wv_grouped = prep.tile([P, PACK, P, PACK], BF16, tag="grouped_w", align_bytes=64)
                 for pair in range(2):
                     turn_words(wv_raw, wv_grouped, pair)
+            if live(r - 3):
+                square_sum(r - 3)
             if live(k - 1):
                 quantise_probs(k - 1)
             if live(r):
                 subtract_top(r)
             if live(r - 1):
                 add_pair(r - 1)
-            if live(k - 2) and units[k - 2][3] == G - 1:
-                store_ctx(k - 2)
             if live(r + 2):
                 copy_odd_head(r + 2, 0)
+            if live(r + 2):
                 copy_odd_head(r + 2, 1)
-            if live(r - 2):
-                square_sum(r - 2)
             if live(r):
                 exponentials(r, 0, 2)
             if live(r + 1):
                 scores(r + 1, EVEN_HEADS, even_ps)
+            if live(k - 1) and units[k - 1][3] == G - 1:
+                attend(k - 1)
+            if now_live:
+                prepare_project(now_b, now_step)
             if now_live:
                 prepare_turns(now_b, now_step)
+            if live(k - 1) and units[k - 1][3] == G - 1:
+                store_ctx(k - 1)
             if live(r):
                 exponentials(r, 2, 4)
             if live(k):
@@ -380,13 +385,9 @@ def tile_sparseattention_pb_t_kernel(tc, q_rot, k_rot, hidden_states, Wv, bv, ou
                 top_of_heads(r + 1)
             if live(k + 1):
                 turn_factor(k + 1)
-            if live(r - 1):
-                sum_heads(r - 1)
-            if now_live:
-                prepare_project(now_b, now_step)
-            if live(k - 1) and units[k - 1][3] == G - 1:
-                attend(k - 1)
-            last = r - 2
+            if live(r - 2):
+                sum_heads(r - 2)
+            last = r - 3
             if live(last) and (last % GROUP == GROUP - 1 or last == n_units - 1):
                 for member in range(last - last % GROUP, last + 1):
                     reciprocal_of_sum(member)

@@ -338,8 +338,6 @@ def tile_sparseattention_pb_t_kernel(tc, q_rot, k_rot, hidden_states, Wv, bv, ou
             now_b, now_step, now_live = prep_at(r)
             old_b, old_step, old_live = prep_at(r - 1)
             k = r - LAG
-            if live(r + 2):
-                scores(r + 2, ODD_HEADS, odd_ps)
             if r == FIRST_ROUND + 1:
                 wv_grouped = prep.tile([P, PACK, P, PACK], BF16, tag="grouped_w", align_bytes=64)
                 for pair in range(2):
@@ -352,22 +350,20 @@ def tile_sparseattention_pb_t_kernel(tc, q_rot, k_rot, hidden_states, Wv, bv, ou
                 subtract_top(r)
             if live(r - 1):
                 add_pair(r - 1)
-            if live(r + 2):
-                copy_odd_head(r + 2, 0)
-            if live(r + 2):
-                copy_odd_head(r + 2, 1)
+            if live(k - 2) and units[k - 2][3] == G - 1:
+                store_ctx(k - 2)
             if live(r):
                 exponentials(r, 0, 2)
             if live(r + 1):
                 scores(r + 1, EVEN_HEADS, even_ps)
-            if live(k - 1) and units[k - 1][3] == G - 1:
-                attend(k - 1)
-            if now_live:
-                prepare_project(now_b, now_step)
+            if live(r + 2):
+                scores(r + 2, ODD_HEADS, odd_ps)
+            if live(r + 2):
+                copy_odd_head(r + 2, 0)
+            if live(r + 2):
+                copy_odd_head(r + 2, 1)
             if now_live:
                 prepare_turns(now_b, now_step)
-            if live(k - 1) and units[k - 1][3] == G - 1:
-                store_ctx(k - 1)
             if live(r):
                 exponentials(r, 2, 4)
             if live(k):
@@ -387,6 +383,10 @@ def tile_sparseattention_pb_t_kernel(tc, q_rot, k_rot, hidden_states, Wv, bv, ou
                 turn_factor(k + 1)
             if live(r - 2):
                 sum_heads(r - 2)
+            if now_live:
+                prepare_project(now_b, now_step)
+            if live(k - 1) and units[k - 1][3] == G - 1:
+                attend(k - 1)
             last = r - 3
             if live(last) and (last % GROUP == GROUP - 1 or last == n_units - 1):
                 for member in range(last - last % GROUP, last + 1):

@@ -83,6 +83,7 @@ def tile_sparseattention_pb_t_kernel(tc, q_rot, k_rot, hidden_states, Wv, bv, ou
         exps = {}
         pair_sums = {}
         sum_banks = {}
+        group_squares = {}
         factors = {}
         factor_banks = {}
         probs_bf = {}
@@ -209,11 +210,11 @@ def tile_sparseattention_pb_t_kernel(tc, q_rot, k_rot, hidden_states, Wv, bv, ou
                     )
                 banks[(k, h)] = bank[:].rearrange("p t i -> p i t")
 
-        def copy_odd_head(k, n):
+        def copy_odd_head(k, n, copy):
             if n == 0:
                 odd = copy_pool.tile([P, 2, P, PACK], F32, tag="odd")
                 odd_copies[k] = odd
-            nc.scalar.copy(out=odd_copies[k][:, n, :, :], in_=banks[(k, ODD_HEADS[n])])
+            copy(out=odd_copies[k][:, n, :, :], in_=banks[(k, ODD_HEADS[n])])
 
         def top_of_pair(k, n):
             if n == 0:
@@ -263,15 +264,21 @@ def tile_sparseattention_pb_t_kernel(tc, q_rot, k_rot, hidden_states, Wv, bv, ou
             sum_banks[k] = bank
 
         def square_sum(k):
-            square = sum_pool.tile([P, PACK, P], F32, tag="square")
-            nc.scalar.activation(out=square[:], in_=sum_banks[k][:], func=ACT.Square)
+            if k % GROUP == 0:
+                squares = sum_pool.tile([P, GROUP, PACK, P], F32, tag="squares", bufs=3)
+                group_squares[k // GROUP] = squares
+            square = group_squares[k // GROUP][:, k % GROUP, :, :]
+            nc.scalar.activation(out=square, in_=sum_banks[k][:], func=ACT.Square)
             factors[k] = square
 
         def reciprocal_of_sum(k):
-            nc.scalar.activation(out=factors[k][:], in_=factors[k][:], func=ACT.Abs_reciprocal_sqrt)
+            nc.scalar.activation(out=factors[k], in_=factors[k], func=ACT.Abs_reciprocal_sqrt)
 
         def turn_factor(k):
-            bank = factor_ps.tile([P, UNIT], F32, tag="factor")
+            if k >= n_units - 8 and k % 2:
+                bank = odd_ps.tile([P, UNIT], F32, tag="scores")
+            else:
+                bank = factor_ps.tile([P, UNIT], F32, tag="factor")
             for c in range(PACK):
                 nc.tensor.transpose(bank[:, c * P : (c + 1) * P], factors[k][:, c, :], ident_f32[:])
             factor_banks[k] = bank
@@ -338,10 +345,6 @@ def tile_sparseattention_pb_t_kernel(tc, q_rot, k_rot, hidden_states, Wv, bv, ou
             now_b, now_step, now_live = prep_at(r)
             old_b, old_step, old_live = prep_at(r - 1)
             k = r - LAG
-            if r == FIRST_ROUND + 1:
-                wv_grouped = prep.tile([P, PACK, P, PACK], BF16, tag="grouped_w", align_bytes=64)
-                for pair in range(2):
-                    turn_words(wv_raw, wv_grouped, pair)
             if live(r - 3):
                 square_sum(r - 3)
             if live(k - 1):
@@ -354,14 +357,16 @@ def tile_sparseattention_pb_t_kernel(tc, q_rot, k_rot, hidden_states, Wv, bv, ou
                 store_ctx(k - 2)
             if live(r):
                 exponentials(r, 0, 2)
-            if live(r + 1):
+            if live(r + 1) and r + 1 > 0:
                 scores(r + 1, EVEN_HEADS, even_ps)
             if live(r + 2):
                 scores(r + 2, ODD_HEADS, odd_ps)
+            if r == FIRST_ROUND:
+                scores(0, EVEN_HEADS, even_ps)
             if live(r + 2):
-                copy_odd_head(r + 2, 0)
-            if live(r + 2):
-                copy_odd_head(r + 2, 1)
+                copy_odd_head(r + 2, 0, nc.scalar.copy)
+            if live(r + 2) and r + 2 >= 8:
+                copy_odd_head(r + 2, 1, nc.scalar.copy)
             if now_live:
                 prepare_turns(now_b, now_step)
             if live(r):
@@ -379,6 +384,8 @@ def tile_sparseattention_pb_t_kernel(tc, q_rot, k_rot, hidden_states, Wv, bv, ou
                 prepare_quantise(old_b, old_step)
             if live(r + 1):
                 top_of_heads(r + 1)
+            if 0 <= r + 2 < 8:
+                copy_odd_head(r + 2, 1, nc.vector.tensor_copy)
             if live(k + 1):
                 turn_factor(k + 1)
             if live(r - 2):
@@ -387,7 +394,11 @@ def tile_sparseattention_pb_t_kernel(tc, q_rot, k_rot, hidden_states, Wv, bv, ou
                 prepare_project(now_b, now_step)
             if live(k - 1) and units[k - 1][3] == G - 1:
                 attend(k - 1)
+            if r == FIRST_ROUND + 1:
+                wv_grouped = prep.tile([P, PACK, P, PACK], BF16, tag="grouped_w", align_bytes=64)
+                for pair in range(2):
+                    turn_words(wv_raw, wv_grouped, pair)
             last = r - 3
             if live(last) and (last % GROUP == GROUP - 1 or last == n_units - 1):
-                for member in range(last - last % GROUP, last + 1):
-                    reciprocal_of_sum(member)
+                squares = group_squares[last // GROUP][:, : last % GROUP + 1, :, :]
+                nc.scalar.activation(out=squares, in_=squares, func=ACT.Abs_reciprocal_sqrt)

from contextlib import ExitStack

import concourse.mybir as mybir
from concourse.masks import make_identity

B, S, D, A, H = 4, 1024, 512, 512, 4
HD = A // H
FLOPS = 2 * B * S * D * A + 2 * 2 * B * H * S * S * HD

F32 = mybir.dt.float32
BF16 = mybir.dt.bfloat16
U32 = mybir.dt.uint32
U8 = mybir.dt.uint8
FP8X4 = mybir.dt.float8_e4m3fn_x4
ACT = mybir.ActivationFunctionType
ALU = mybir.AluOpType

P = 128
PACK = 4
K_PASS = P * PACK
G = S // K_PASS
TILES = G * PACK
UNIT = P * PACK
UNITS_PER_BATCH = TILES * G
GROUP = 4
LAG = GROUP + 4
PREP_LEAD = 6
HEAD_STEPS = TILES
WORD_STEP = 4
V_STEP = TILES
PREP_STEPS = V_STEP + G * H
FIRST_ROUND = -2
EVEN_HEADS = (0, 2)
ODD_HEADS = (1, 3)
SLOT = {0: 0, 2: 1, 1: 2, 3: 3}
QK_AHEAD = 4


def tile_sparseattention_pb_t_kernel(tc, q_rot, k_rot, hidden_states, Wv, bv, out):
    nc = tc.nc
    units = [(b, gi, ti, g) for b in range(B) for gi in range(G) for g in range(G) for ti in range(PACK)]
    n_units = len(units)

    with ExitStack() as stack:
        const = stack.enter_context(tc.tile_pool(name="const", bufs=1))
        raw_pool = stack.enter_context(tc.tile_pool(name="raw", bufs=QK_AHEAD))
        prep = stack.enter_context(tc.tile_pool(name="prep", bufs=1))
        per_batch = stack.enter_context(tc.tile_pool(name="per_batch", bufs=2))
        soft = stack.enter_context(tc.tile_pool(name="soft", bufs=2))
        copy_pool = stack.enter_context(tc.tile_pool(name="copies", bufs=3))
        pair_pool = stack.enter_context(tc.tile_pool(name="pairs", bufs=2))
        exp_pool = stack.enter_context(tc.tile_pool(name="exp", bufs=LAG + 1))
        sum_pool = stack.enter_context(tc.tile_pool(name="sum", bufs=LAG + 1))
        code_pool = stack.enter_context(tc.tile_pool(name="codes", bufs=PACK + 2))
        out_pool = stack.enter_context(tc.tile_pool(name="out", bufs=2))
        even_ps = stack.enter_context(tc.psum_pool(name="even_ps", bufs=2))
        odd_ps = stack.enter_context(tc.psum_pool(name="odd_ps", bufs=2))
        sum_ps = stack.enter_context(tc.psum_pool(name="sum_ps", bufs=1))
        factor_ps = stack.enter_context(tc.psum_pool(name="factor_ps", bufs=1))
        other_ps = stack.enter_context(tc.psum_pool(name="other_ps", bufs=2))
        stack.enter_context(tc.manual_schedule())

        ident_bf = const.tile([P, P], BF16)
        make_identity(nc, ident_bf[:])
        ident_f32 = const.tile([P, P], F32)
        make_identity(nc, ident_f32[:])
        bias_rows = const.tile([P, A], BF16)
        wv_codes = const.tile([P, A], U32, align_bytes=64)
        wv_scales = const.tile([P, A], U8, align_bytes=64)

        qk_raws = {}
        h_raws = {}
        turned_qk = {}
        hs_mx = {}
        grouped_hs = {}
        v_banks = {}
        grouped_v = {}
        v_mx = {}
        banks = {}
        odd_copies = {}
        pair_tops = {}
        tops = {}
        exps = {}
        pair_sums = {}
        sum_banks = {}
        group_squares = {}
        factors = {}
        factor_banks = {}
        probs_bf = {}
        probs_mx = {}
        ctx_banks = {}

        def load_qk(n):
            b, tile_index = divmod(n, TILES)
            if b < B:
                g, t = divmod(tile_index, PACK)
                pair = []
                for name, x in (("k", k_rot), ("q", q_rot)):
                    raw = raw_pool.tile([P, D], BF16, tag="raw_" + name, name="raw_" + name)
                    nc.sync.dma_start(out=raw[:], in_=x[b].rearrange("(g p t) c -> g t p c", g=G, p=P)[g, t])
                    pair.append(raw)
                qk_raws[(b, tile_index)] = pair

        def load_hidden(b):
            if b < B:
                for g in range(G):
                    raw = raw_pool.tile([P, PACK, D], BF16, tag="raw_h", name="raw_h", bufs=G)
                    nc.sync.dma_start(out=raw[:], in_=hidden_states[b].rearrange("(g p t) c -> g p t c", g=G, p=P)[g])
                    h_raws[(b, g)] = raw

        def turn_words(raw, grouped, pair):
            words = raw[:].bitcast(F32)
            turned = other_ps.tile([P, 2, 2, P], F32, tag="other")
            for n in range(2):
                for u in range(2):
                    nc.tensor.transpose(turned[:, n, u, :], words[:, 2 * pair + n, u * P : (u + 1) * P], ident_f32[:])
            nc.scalar.copy(
                out=grouped[:].bitcast(F32)[:, 2 * pair : 2 * pair + 2, :, :],
                in_=turned[:].rearrange("p n u r -> p n r u"),
            )

        def turn_heads(b, tile_index):
            g, t = divmod(tile_index, PACK)
            if tile_index == 0:
                qk = per_batch.tile([P, G, PACK, 2, H, P], BF16, tag="turned_qk")
                turned_qk[b] = qk
            k_raw, q_raw = qk_raws[(b, tile_index)]
            turned = other_ps.tile([P, 2, H, P], BF16, tag="other")
            for which, raw in enumerate((q_raw, k_raw)):
                for h in range(H):
                    nc.tensor.transpose(turned[:, which, h, :], raw[:, h * HD : (h + 1) * HD], ident_bf[:])
            nc.scalar.copy(out=turned_qk[b][:, g, t, :, :, :], in_=turned[:])
            load_qk(b * TILES + tile_index + QK_AHEAD)

        def quantise_grouped(grouped, codes, scales):
            nc.vector.quantize_mx(
                out=codes.bitcast(FP8X4), scales=scales, in_=grouped[:].rearrange("p n r t -> p (n r t)")
            )

        def project_v(b, g, h):
            codes, scales = hs_mx[b]
            bank = other_ps.tile([P, PACK, HD], F32, tag="other")
            for t in range(PACK):
                nc.tensor.matmul_mx(
                    out=bank[:, t, :],
                    lhsT=codes[:, g, t * P : (t + 1) * P].bitcast(FP8X4),
                    lhsT_scale=scales[:, g, t * P : (t + 1) * P],
                    rhs=wv_codes[:, h * HD : (h + 1) * HD].bitcast(FP8X4),
                    rhs_scale=wv_scales[:, h * HD : (h + 1) * HD],
                    start=True,
                    stop=True,
                )
            v_banks[(b, g, h)] = bank

        def prepare_turns(b, step):
            if step < HEAD_STEPS:
                turn_heads(b, step)
            if WORD_STEP <= step < WORD_STEP + 2 * G:
                g, pair = divmod(step - WORD_STEP, 2)
                if pair == 0:
                    grouped = prep.tile([P, PACK, P, PACK], BF16, tag="grouped", bufs=2, align_bytes=64)
                    grouped_hs[(b, g)] = grouped
                turn_words(h_raws[(b, g)], grouped_hs[(b, g)], pair)
                if step == WORD_STEP + 2 * G - 1:
                    load_hidden(b + 1)

        def prepare_project(b, step):
            if step >= V_STEP:
                g, h = divmod(step - V_STEP, H)
                project_v(b, g, h)

        def prepare_add(b, step):
            if step >= V_STEP:
                g, h = divmod(step - V_STEP, H)
                if h == 0:
                    grouped = prep.tile([P, H, HD, PACK], BF16, tag="grouped_v", align_bytes=64)
                    grouped_v[(b, g)] = grouped
                nc.vector.tensor_tensor(
                    out=grouped_v[(b, g)][:, h, :, :],
                    in0=v_banks[(b, g, h)][:].rearrange("p t a -> p a t"),
                    in1=bias_rows[:, h * HD : (h + 1) * HD].unsqueeze(2).to_broadcast([P, HD, PACK]),
                    op=ALU.add,
                )

        def prepare_quantise(b, step):
            if WORD_STEP <= step < WORD_STEP + 2 * G and (step - WORD_STEP) % 2 == 1:
                g = (step - WORD_STEP) // 2
                if g == 0:
                    hs_codes = prep.tile([P, G, K_PASS], U32, align_bytes=64)
                    hs_scales = prep.tile([P, G, K_PASS], U8, align_bytes=64)
                    hs_mx[b] = (hs_codes, hs_scales)
                quantise_grouped(grouped_hs[(b, g)], hs_mx[b][0][:, g, :], hs_mx[b][1][:, g, :])
            if step >= V_STEP:
                g, h = divmod(step - V_STEP, H)
                if h == H - 1:
                    if g == 0:
                        v_codes = per_batch.tile([P, G, A], U32, align_bytes=64)
                        v_scales = per_batch.tile([P, G, A], U8, align_bytes=64)
                        v_mx[b] = (v_codes, v_scales)
                    quantise_grouped(grouped_v[(b, g)], v_mx[b][0][:, g, :], v_mx[b][1][:, g, :])

        def scores(k, heads, pool):
            b, gi, ti, g = units[k]
            qk = turned_qk[b]
            for h in heads:
                bank = pool.tile([P, PACK, P], F32, tag="scores")
                for t in range(PACK):
                    nc.tensor.matmul(
                        out=bank[:, t, :], lhsT=qk[:, g, t, 1, h, :], rhs=qk[:, gi, ti, 0, h, :], start=True, stop=True
                    )
                banks[(k, h)] = bank[:].rearrange("p t i -> p i t")

        def copy_odd_head(k, n, copy):
            if n == 0:
                odd = copy_pool.tile([P, 2, P, PACK], F32, tag="odd")
                odd_copies[k] = odd
            copy(out=odd_copies[k][:, n, :, :], in_=banks[(k, ODD_HEADS[n])])

        def top_of_pair(k, n):
            if n == 0:
                pair_top = soft.tile([P, 2, P, PACK], BF16, tag="pair_top")
                pair_tops[k] = pair_top
            nc.vector.tensor_tensor(
                out=pair_tops[k][:, n, :, :], in0=banks[(k, EVEN_HEADS[n])], in1=odd_copies[k][:, n, :, :], op=ALU.max
            )

        def top_of_heads(k):
            top = soft.tile([P, P, PACK], BF16, tag="top")
            nc.vector.tensor_tensor(out=top[:], in0=pair_tops[k][:, 0, :, :], in1=pair_tops[k][:, 1, :, :], op=ALU.max)
            tops[k] = top

        def subtract_top(k):
            shifted = exp_pool.tile([P, H, P, PACK], F32, tag="exps")
            for h in EVEN_HEADS:
                nc.vector.tensor_tensor(out=shifted[:, SLOT[h], :, :], in0=banks[(k, h)], in1=tops[k][:], op=ALU.subtract)
            for n, h in enumerate(ODD_HEADS):
                nc.gpsimd.tensor_tensor(
                    out=shifted[:, SLOT[h], :, :], in0=odd_copies[k][:, n, :, :], in1=tops[k][:], op=ALU.subtract
                )
            exps[k] = shifted[:].rearrange("p h i t -> p h (i t)")

        def exponentials(k, first, last):
            part = exps[k][:, first:last, :]
            nc.scalar.activation(out=part, in_=part, func=ACT.Exp)

        def add_pair(k):
            pair = pair_pool.tile([P, UNIT], F32, tag="pair")
            nc.gpsimd.tensor_tensor(out=pair[:], in0=exps[k][:, 0, :], in1=exps[k][:, 1, :], op=ALU.add)
            pair_sums[k] = pair

        def sum_heads(k):
            parts = (pair_sums[k][:], exps[k][:, 2, :], exps[k][:, 3, :])
            bank = sum_ps.tile([P, PACK, P], F32, tag="sum")
            for c in range(PACK):
                for n, part in enumerate(parts):
                    nc.tensor.matmul(
                        out=bank[:, c, :],
                        lhsT=part[:, c * P : (c + 1) * P],
                        rhs=ident_f32[:],
                        start=(n == 0),
                        stop=(n == len(parts) - 1),
                        is_transpose=True,
                    )
            sum_banks[k] = bank

        def square_sum(k):
            if k % GROUP == 0:
                squares = sum_pool.tile([P, GROUP, PACK, P], F32, tag="squares", bufs=3)
                group_squares[k // GROUP] = squares
            square = group_squares[k // GROUP][:, k % GROUP, :, :]
            nc.scalar.activation(out=square, in_=sum_banks[k][:], func=ACT.Square)
            factors[k] = square

        def reciprocal_of_sum(k):
            nc.scalar.activation(out=factors[k], in_=factors[k], func=ACT.Abs_reciprocal_sqrt)

        def turn_factor(k):
            if k >= n_units - 8 and k % 2:
                bank = odd_ps.tile([P, UNIT], F32, tag="scores")
            else:
                bank = factor_ps.tile([P, UNIT], F32, tag="factor")
            for c in range(PACK):
                nc.tensor.transpose(bank[:, c * P : (c + 1) * P], factors[k][:, c, :], ident_f32[:])
            factor_banks[k] = bank

        def normalise(k):
            probs = soft.tile([P, H, UNIT], BF16, tag="probs", align_bytes=64)
            nc.vector.tensor_tensor(
                out=probs[:],
                in0=exps[k][:],
                in1=factor_banks[k][:].unsqueeze(1).to_broadcast([P, H, UNIT]),
                op=ALU.mult,
            )
            probs_bf[k] = probs

        def quantise_probs(k):
            codes = code_pool.tile([P, H * P], U32, tag="probs_codes", align_bytes=64)
            scales = code_pool.tile([P, H * P], U8, tag="probs_scales", align_bytes=64)
            nc.vector.quantize_mx(
                out=codes[:].bitcast(FP8X4), scales=scales[:], in_=probs_bf[k][:].rearrange("p h x -> p (h x)")
            )
            probs_mx[k] = (codes, scales)

        def attend(k):
            v_codes, v_scales = v_mx[units[k][0]]
            ctx = other_ps.tile([P, H, HD], F32, tag="other")
            for h in range(H):
                n = SLOT[h]
                for g in range(G):
                    codes, scales = probs_mx[k - (G - 1 - g) * PACK]
                    nc.tensor.matmul_mx(
                        out=ctx[:, h, :],
                        lhsT=codes[:, n * P : (n + 1) * P].bitcast(FP8X4),
                        lhsT_scale=scales[:, n * P : (n + 1) * P],
                        rhs=v_codes[:, g, h * HD : (h + 1) * HD].bitcast(FP8X4),
                        rhs_scale=v_scales[:, g, h * HD : (h + 1) * HD],
                        start=(g == 0),
                        stop=(g == G - 1),
                    )
            ctx_banks[k] = ctx

        def store_ctx(k):
            b, gi, ti, last_pass = units[k]
            rows = out_pool.tile([P, H, HD], F32, tag="rows")
            nc.scalar.copy(out=rows[:], in_=ctx_banks[k][:])
            nc.sync.dma_start(out=out[b].rearrange("(h g m) (t d) -> g t m h d", h=H, g=G, t=PACK)[gi, ti], in_=rows[:])

        for n in range(QK_AHEAD):
            load_qk(n)
        wv_raw = prep.tile([P, PACK, D], BF16, tag="grouped_v", align_bytes=64)
        nc.sync.dma_start(out=wv_raw[:], in_=Wv.rearrange("(n p) c -> p n c", p=P))
        load_hidden(0)
        nc.sync.dma_start(out=bias_rows[:], in_=bv.partition_broadcast(P))
        for step in range(FIRST_ROUND + PREP_LEAD):
            prepare_turns(0, step)

        def live(k):
            return 0 <= k < n_units

        def prep_at(r):
            b, step = divmod(r + PREP_LEAD, UNITS_PER_BATCH)
            return b, step, b < B

        for r in range(FIRST_ROUND, n_units + LAG + 3):
            now_b, now_step, now_live = prep_at(r)
            old_b, old_step, old_live = prep_at(r - 1)
            k = r - LAG
            if live(r - 3):
                square_sum(r - 3)
            if live(k - 1):
                quantise_probs(k - 1)
            if live(r):
                subtract_top(r)
            if live(r - 1):
                add_pair(r - 1)
            if live(k - 2) and units[k - 2][3] == G - 1:
                store_ctx(k - 2)
            if live(r):
                exponentials(r, 0, 2)
            if live(r + 1) and r + 1 > 0:
                scores(r + 1, EVEN_HEADS, even_ps)
            if live(r + 2):
                scores(r + 2, ODD_HEADS, odd_ps)
            if r == FIRST_ROUND:
                scores(0, EVEN_HEADS, even_ps)
            if live(r + 2):
                copy_odd_head(r + 2, 0, nc.scalar.copy)
            if live(r + 2) and r + 2 >= 8:
                copy_odd_head(r + 2, 1, nc.scalar.copy)
            if now_live:
                prepare_turns(now_b, now_step)
            if live(r):
                exponentials(r, 2, 4)
            if live(k):
                normalise(k)
            if live(r + 1):
                top_of_pair(r + 1, 0)
                top_of_pair(r + 1, 1)
            if old_live:
                prepare_add(old_b, old_step)
            if r == FIRST_ROUND + 2:
                quantise_grouped(wv_grouped, wv_codes[:], wv_scales[:])
            if old_live:
                prepare_quantise(old_b, old_step)
            if live(r + 1):
                top_of_heads(r + 1)
            if 0 <= r + 2 < 8:
                copy_odd_head(r + 2, 1, nc.vector.tensor_copy)
            if live(k + 1):
                turn_factor(k + 1)
            if live(r - 2):
                sum_heads(r - 2)
            if now_live:
                prepare_project(now_b, now_step)
            if live(k - 1) and units[k - 1][3] == G - 1:
                attend(k - 1)
            if r == FIRST_ROUND + 1:
                wv_grouped = prep.tile([P, PACK, P, PACK], BF16, tag="grouped_w", align_bytes=64)
                for pair in range(2):
                    turn_words(wv_raw, wv_grouped, pair)
            last = r - 3
            if live(last) and (last % GROUP == GROUP - 1 or last == n_units - 1):
                squares = group_squares[last // GROUP][:, : last % GROUP + 1, :, :]
                nc.scalar.activation(out=squares, in_=squares, func=ACT.Abs_reciprocal_sqrt)
